import numpy as np
import ml_dtypes


def mxq(x, axis, fmt="e4m3"):
    dtype, down = {"e4m3": (ml_dtypes.float8_e4m3fn, 7), "e5m2": (ml_dtypes.float8_e5m2, 14)}[fmt]
    v = np.moveaxis(np.asarray(x, np.float32).astype(ml_dtypes.bfloat16).astype(np.float64), axis, -1)
    blocks = v.reshape(v.shape[:-1] + (-1, 32))
    amax = np.abs(blocks).max(-1, keepdims=True)
    byte = np.maximum(np.where(amax > 0, np.frexp(amax)[1] - 1 + 127, 0) - down, 1)
    scale = np.exp2(byte - 127.0)
    codes = (blocks / scale).astype(np.float32).astype(dtype).astype(np.float64)
    return np.moveaxis((codes * scale).reshape(v.shape), -1, axis)


WIDE = False


def mx_kscale(k):
    if not WIDE:
        return np.ones(k)
    levels = np.array([10, -10, 5, -5, 0])
    a = np.random.permutation(np.resize(levels, k // 512 * 4)).reshape(k // 512, 4)
    idx = np.arange(k)
    return np.exp2(a[idx // 512, idx % 128 // 32])


BF16 = ml_dtypes.bfloat16


def bf(x):
    return np.asarray(x, np.float32).astype(BF16)


def f64(x):
    return np.asarray(x).astype(np.float64)


E2M1 = np.array([0.0, 0.5, 1.0, 1.5, 2.0, 3.0, 4.0, 6.0, -0.0, -0.5, -1.0, -1.5, -2.0, -3.0, -4.0, -6.0])


def pack_weight(w, fmt):
    k, n = w.shape
    w = f64(bf(w)).reshape(k // 32, 32, n)
    amax = np.abs(w).max(1)
    if fmt == "e4m3":
        byte = np.frexp(amax)[1] - 1 + 127 - 7
    else:
        mant, ex = np.frexp(amax / 6.0)
        byte = np.where(mant > 0.5, ex, ex - 1) + 127
    byte = np.clip(np.where(amax > 0, byte, 1), 1, 254)
    scaled = (w * np.exp2(127.0 - byte)[:, None, :]).reshape(k, n).astype(np.float32)
    by_word = np.ascontiguousarray(scaled.reshape(k // 512, 128, 4, n).transpose(0, 1, 3, 2))
    if fmt == "e4m3":
        words = by_word.astype(ml_dtypes.float8_e4m3fn).view(np.uint8)
    else:
        c = by_word.astype(ml_dtypes.float4_e2m1fn).view(np.uint8) & 0xF
        words = c[..., 0::2] | (c[..., 1::2] << 4)
    return np.ascontiguousarray(words), np.ascontiguousarray(byte.astype(np.uint8).reshape(k // 512, 16, n))


def unpack_weight(words, scales, fmt):
    g, p, n, _ = words.shape
    if fmt == "e4m3":
        vals = np.ascontiguousarray(words).view(ml_dtypes.float8_e4m3fn).astype(np.float64)
    else:
        nib = np.empty((g, p, n, 4), np.uint8)
        nib[..., 0::2] = words & 0xF
        nib[..., 1::2] = words >> 4
        vals = E2M1[nib]
    vals = vals * np.repeat(np.exp2(scales.astype(np.float64) - 127.0), 8, axis=1)[..., None]
    return vals.transpose(0, 1, 3, 2).reshape(g * 512, n)


B, IN, H = 128, 2048, 1536
FMT = "e4m3"


def hard_sigmoid(v):
    return np.clip(v / 6.0 + 0.5, 0.0, 1.0)


def hard_tanh(v):
    return np.clip(v, -1.0, 1.0)


def setup_inputs():
    s, t = mx_kscale(IN), mx_kscale(H)
    input_ = bf(np.random.standard_normal((B, IN)) * s)
    h_0 = bf(np.random.standard_normal((B, H)) * t)
    c_0 = bf(np.random.standard_normal((B, H)))
    W_ih = np.random.standard_normal((4 * H, IN)) * 1.25 / np.sqrt(IN) / s[None, :]
    W_hh = np.random.standard_normal((4 * H, H)) * 1.25 / np.sqrt(H) / t[None, :]
    b_hh = bf(np.random.standard_normal(4 * H) * 0.3)
    W_ih_words, W_ih_scales = pack_weight(np.ascontiguousarray(W_ih.T), FMT)
    W_hh_words, W_hh_scales = pack_weight(np.ascontiguousarray(W_hh.T), FMT)
    return {"input_": input_,
            "h_0": h_0,
            "c_0": c_0,
            "W_ih_words": W_ih_words,
            "W_ih_scales": W_ih_scales,
            "W_hh_words": W_hh_words,
            "W_hh_scales": W_hh_scales,
            "b_hh": b_hh}


def reference(input_, h_0, c_0, W_ih_words, W_ih_scales, W_hh_words, W_hh_scales, b_hh):
    wi = mxq(f64(input_), 1, "e4m3") @ unpack_weight(W_ih_words, W_ih_scales, FMT)
    wh_b = (mxq(f64(h_0), 1, "e4m3") @ unpack_weight(W_hh_words, W_hh_scales, FMT)) + f64(b_hh)
    h_x4 = wh_b + wi
    f, i, o, g = np.split(h_x4, 4, axis=1)
    new = hard_sigmoid(i) * hard_tanh(g)
    old = hard_sigmoid(f) * f64(c_0)
    c_1 = old + new
    h_1 = hard_sigmoid(o) * hard_tanh(c_1)
    return (h_1, c_1)

@@ -1,0 +1,185 @@
+from contextlib import ExitStack
+
+import concourse.mybir as mybir
+from concourse.masks import make_identity
+
+F32 = mybir.dt.float32
+BF16 = mybir.dt.bfloat16
+I32 = mybir.dt.int32
+U32 = mybir.dt.uint32
+U8 = mybir.dt.uint8
+FP8X4 = mybir.dt.float8_e4m3fn_x4
+ALU = mybir.AluOpType
+
+P = 128
+B = 128
+IN = 2048
+H = 1536
+NG = 4 * H
+PASSES_IH = IN // 512
+PASSES = (IN + H) // 512
+BANK = 512
+W_BUFS = 20
+FLOPS = 2 * B * (IN + H) * NG
+
+COL_F, COL_I, COL_O, COL_G = 0, H, 2 * H, 3 * H
+
+
+def tile_qlstmcell_w_kernel(
+    tc, input_, h_0, c_0, W_ih_words, W_ih_scales, W_hh_words, W_hh_scales, b_hh, out_0, out_1
+):
+    nc = tc.nc
+    with ExitStack() as ctx:
+        keep = ctx.enter_context(tc.tile_pool(name="keep", bufs=1))
+        wpool = ctx.enter_context(tc.tile_pool(name="wpool", bufs=W_BUFS))
+        psum = ctx.enter_context(tc.psum_pool(name="psum", bufs=8))
+
+        planes_ih = keep.tile([P, NG], U8, align_bytes=64)
+        planes_hh = keep.tile([P, NG], U8, align_bytes=64)
+        nc.vector.memset(planes_ih[:].bitcast(I32), 0)
+        nc.vector.memset(planes_hh[:].bitcast(I32), 0)
+
+        xh = keep.tile([P, IN + H], BF16, align_bytes=64)
+        nc.sync.dma_start(out=xh[:, 0:IN], in_=input_)
+        nc.sync.dma_start(out=xh[:, IN : IN + H], in_=h_0)
+
+        for q in range(4):
+            nc.sync.dma_start(
+                out=planes_ih[32 * q : 32 * q + 16, :].bitcast(I32),
+                in_=W_ih_scales[:, 4 * q : 4 * q + 4, :].bitcast(I32),
+            )
+        for q in range(4):
+            nc.sync.dma_start(
+                out=planes_hh[32 * q : 32 * q + 12, :].bitcast(I32),
+                in_=W_hh_scales[:, 4 * q : 4 * q + 4, :].bitcast(I32),
+            )
+
+        ident = keep.tile([P, P], F32)
+        make_identity(nc, ident[:])
+
+        brow = keep.tile([P, NG], BF16)
+        nc.vector.memset(brow[:].bitcast(I32), 0)
+        ones = keep.tile([P, P], BF16)
+        nc.vector.memset(ones[:], 1.0)
+        nc.scalar.dma_start(out=brow[0:1, :], in_=b_hh.rearrange("(o n) -> o n", o=1))
+        c0_sb = keep.tile([P, H], BF16)
+        nc.scalar.dma_start(out=c0_sb[:], in_=c_0)
+
+        xh_words = xh[:].bitcast(F32)
+        grouped = keep.tile([P, PASSES, B, 4], BF16, align_bytes=64)
+        xq = keep.tile([P, PASSES, B], U32, align_bytes=64)
+        xs = keep.tile([P, PASSES, B], U8, align_bytes=64)
+        for first in range(0, PASSES, 2):
+            n = min(2, PASSES - first)
+            xt = psum.tile([P, 2, 2, B], F32, tag="bank")
+            for j in range(n):
+                g = first + j
+                for u in range(2):
+                    nc.tensor.transpose(
+                        xt[:, j, u, :], xh_words[:, 256 * g + u : 256 * (g + 1) : 2], ident[:]
+                    )
+            nc.vector.tensor_copy(
+                out=grouped[:, first : first + n].bitcast(F32),
+                in_=xt[:, 0:n].rearrange("p g u r -> p g r u"),
+            )
+            nc.vector.quantize_mx(
+                out=xq[:, first : first + n, :].rearrange("p g r -> p (g r)").bitcast(FP8X4),
+                scales=xs[:, first : first + n, :].rearrange("p g r -> p (g r)"),
+                in_=grouped[:, first : first + n].rearrange("p g r t -> p (g r t)"),
+            )
+
+        bias = keep.tile([P, NG], BF16)
+        for base in (COL_F, COL_I, COL_G, COL_O):
+            for c in range(base, base + H, BANK):
+                pb = psum.tile([P, BANK], F32, tag="bank")
+                nc.tensor.matmul(out=pb[:], lhsT=ones[:], rhs=brow[:, c : c + BANK], start=True, stop=True)
+                nc.scalar.copy(out=bias[:, c : c + BANK], in_=pb[:])
+
+        def load(g, c_lo, c_hi):
+            words = W_ih_words[g] if g < PASSES_IH else W_hh_words[g - PASSES_IH]
+            wt = wpool.tile([P, H], U32, tag="w", align_bytes=64)
+            nc.sync.dma_start(
+                out=wt[:, 0 : c_hi - c_lo].bitcast(I32),
+                in_=words.rearrange("p n t -> p (n t)")[:, 4 * c_lo : 4 * c_hi].bitcast(I32),
+            )
+            return wt
+
+        def mx_pass(acc, g, wt, off, col, n):
+            planes = planes_ih if g < PASSES_IH else planes_hh
+            k = 4 * (g % PASSES_IH)
+            nc.tensor.matmul_mx(
+                out=acc[:, 0:n],
+                lhsT=xq[:, g, :].bitcast(FP8X4),
+                lhsT_scale=xs[:, g, :],
+                rhs=wt[:, off : off + n].bitcast(FP8X4),
+                rhs_scale=planes[k:P, col : col + n],
+                start=(g == 0),
+                stop=(g == PASSES - 1),
+            )
+
+        def gate(base, widths, dest, lo, hi, after):
+            offs = [sum(widths[:i]) for i in range(len(widths))]
+            accs = [psum.tile([P, BANK], F32, tag="bank", name="acc") for w in widths]
+            for g in range(PASSES - 1):
+                wt = load(g, base, base + H)
+                for acc, off, n in zip(accs, offs, widths):
+                    mx_pass(acc, g, wt, off, base + off, n)
+            g = PASSES - 1
+            if after is None:
+                wt = load(g, base, base + H)
+            for acc, off, n in zip(accs, offs, widths):
+                if after is None:
+                    mx_pass(acc, g, wt, off, base + off, n)
+                else:
+                    part = load(g, base + off, base + off + n)
+                    mx_pass(acc, g, part, 0, base + off, n)
+                nc.vector.tensor_tensor(
+                    out=dest[:, off : off + n],
+                    in0=acc[:, 0:n],
+                    in1=bias[:, base + off : base + off + n],
+                    op=ALU.add,
+                )
+                if after is not None:
+                    nc.vector.tensor_scalar(
+                        out=dest[:, off : off + n], in0=dest[:, off : off + n],
+                        scalar1=lo, scalar2=hi, op0=ALU.max, op1=ALU.min,
+                    )
+                    after(off, n)
+            if after is None:
+                nc.vector.tensor_scalar(
+                    out=dest[:], in0=dest[:], scalar1=lo, scalar2=hi, op0=ALU.max, op1=ALU.min
+                )
+
+        three = [BANK, BANK, BANK]
+        acc_c = keep.tile([P, H], F32)
+        gate(COL_F, three, acc_c, -3.0, 3.0, None)
+        nc.vector.scalar_tensor_tensor(
+            out=acc_c[:], in0=acc_c[:], scalar=3.0, in1=c0_sb[:], op0=ALU.add, op1=ALU.mult
+        )
+        gi = keep.tile([P, H], F32)
+        gate(COL_I, three, gi, -3.0, 3.0, None)
+        gg = keep.tile([P, H], F32)
+        gate(COL_G, three, gg, -1.0, 1.0, None)
+        nc.vector.scalar_tensor_tensor(
+            out=gg[:], in0=gi[:], scalar=3.0, in1=gg[:], op0=ALU.add, op1=ALU.mult
+        )
+        nc.vector.tensor_tensor(out=acc_c[:], in0=acc_c[:], in1=gg[:], op=ALU.add)
+        c1 = keep.tile([P, H], F32)
+        nc.vector.tensor_scalar(out=c1[:], in0=acc_c[:], scalar1=1.0 / 6.0, scalar2=None, op0=ALU.mult)
+        nc.scalar.dma_start(out=out_1, in_=c1[:])
+        th = keep.tile([P, H], F32)
+        nc.vector.tensor_scalar(
+            out=th[:], in0=acc_c[:], scalar1=-6.0, scalar2=6.0, op0=ALU.max, op1=ALU.min
+        )
+        nc.vector.tensor_scalar(out=th[:], in0=th[:], scalar1=1.0 / 36.0, scalar2=None, op0=ALU.mult)
+
+        go = keep.tile([P, H], F32)
+
+        def finish(off, n):
+            nc.vector.scalar_tensor_tensor(
+                out=go[:, off : off + n], in0=go[:, off : off + n], scalar=3.0,
+                in1=th[:, off : off + n], op0=ALU.add, op1=ALU.mult,
+            )
+            nc.sync.dma_start(out=out_0[:, off : off + n], in_=go[:, off : off + n])
+
+        gate(COL_O, [BANK, BANK, 256, 256], go, -3.0, 3.0, finish)

@@ -34,6 +34,9 @@ def tile_qlstmcell_w_kernel(
         wpool = ctx.enter_context(tc.tile_pool(name="wpool", bufs=W_BUFS))
         psum = ctx.enter_context(tc.psum_pool(name="psum", bufs=8))
 
+        ident = keep.tile([P, P], F32)
+        make_identity(nc, ident[:])
+
         planes_ih = keep.tile([P, NG], U8, align_bytes=64)
         planes_hh = keep.tile([P, NG], U8, align_bytes=64)
         nc.vector.memset(planes_ih[:].bitcast(I32), 0)
@@ -44,18 +47,15 @@ def tile_qlstmcell_w_kernel(
         nc.sync.dma_start(out=xh[:, IN : IN + H], in_=h_0)
 
         for q in range(4):
-            nc.sync.dma_start(
-                out=planes_ih[32 * q : 32 * q + 16, :].bitcast(I32),
-                in_=W_ih_scales[:, 4 * q : 4 * q + 4, :].bitcast(I32),
+            nc.gpsimd.dma_start(
+                out=planes_ih[32 * q : 32 * q + 16, :].bitcast(F32),
+                in_=W_ih_scales[:, 4 * q : 4 * q + 4, :].bitcast(F32),
             )
         for q in range(4):
-            nc.sync.dma_start(
-                out=planes_hh[32 * q : 32 * q + 12, :].bitcast(I32),
-                in_=W_hh_scales[:, 4 * q : 4 * q + 4, :].bitcast(I32),
+            nc.gpsimd.dma_start(
+                out=planes_hh[32 * q : 32 * q + 12, :].bitcast(F32),
+                in_=W_hh_scales[:, 4 * q : 4 * q + 4, :].bitcast(F32),
             )
-
-        ident = keep.tile([P, P], F32)
-        make_identity(nc, ident[:])
 
         brow = keep.tile([P, NG], BF16)
         nc.vector.memset(brow[:].bitcast(I32), 0)

@@ -17,7 +17,8 @@ IN = 2048
 H = 1536
 NG = 4 * H
 PASSES_IH = IN // 512
-PASSES = (IN + H) // 512
+PASSES_HH = H // 512
+PASSES = PASSES_IH + PASSES_HH
 BANK = 512
 W_BUFS = 20
 FLOPS = 2 * B * (IN + H) * NG
@@ -88,6 +89,9 @@ def tile_qlstmcell_w_kernel(
                 in_=grouped[:, first : first + n].rearrange("p g r t -> p (g r t)"),
             )
 
+        c0s = keep.tile([P, H], F32)
+        nc.vector.tensor_scalar(out=c0s[:], in0=c0_sb[:], scalar1=1.0 / 36.0, scalar2=None, op0=ALU.mult)
+
         bias = keep.tile([P, NG], BF16)
         for base in (COL_F, COL_I, COL_G, COL_O):
             for c in range(base, base + H, BANK):
@@ -104,6 +108,15 @@ def tile_qlstmcell_w_kernel(
             )
             return wt
 
+        def load_hh(c_lo, c_hi):
+            n = c_hi - c_lo
+            wt = wpool.tile([P, H], U32, tag="w", align_bytes=64)
+            nc.sync.dma_start(
+                out=wt[:, 0 : PASSES_HH * n].rearrange("p (g n) -> p g n", g=PASSES_HH).bitcast(I32),
+                in_=W_hh_words.rearrange("g p n t -> p g (n t)")[:, :, 4 * c_lo : 4 * c_hi].bitcast(I32),
+            )
+            return wt
+
         def mx_pass(acc, g, wt, off, col, n):
             planes = planes_ih if g < PASSES_IH else planes_hh
             k = 4 * (g % PASSES_IH)
@@ -117,69 +130,64 @@ def tile_qlstmcell_w_kernel(
                 stop=(g == PASSES - 1),
             )
 
-        def gate(base, widths, dest, lo, hi, after):
+        def gate(base, widths, whole_passes, dest, lo, hi, after):
             offs = [sum(widths[:i]) for i in range(len(widths))]
             accs = [psum.tile([P, BANK], F32, tag="bank", name="acc") for w in widths]
-            for g in range(PASSES - 1):
+            for g in range(whole_passes):
                 wt = load(g, base, base + H)
                 for acc, off, n in zip(accs, offs, widths):
                     mx_pass(acc, g, wt, off, base + off, n)
-            g = PASSES - 1
-            if after is None:
-                wt = load(g, base, base + H)
+            if whole_passes < PASSES:
+                for acc, off, n in zip(accs, offs, widths):
+                    part = load_hh(base + off, base + off + n)
+                    for g in range(PASSES_IH, PASSES):
+                        mx_pass(acc, g, part, (g - PASSES_IH) * n, base + off, n)
+                nc.sync.dma_start(out=out_1, in_=c1[:])
             for acc, off, n in zip(accs, offs, widths):
-                if after is None:
-                    mx_pass(acc, g, wt, off, base + off, n)
-                else:
-                    part = load(g, base + off, base + off + n)
-                    mx_pass(acc, g, part, 0, base + off, n)
+                piece = dest[:, off : off + n]
                 nc.vector.tensor_tensor(
-                    out=dest[:, off : off + n],
-                    in0=acc[:, 0:n],
-                    in1=bias[:, base + off : base + off + n],
-                    op=ALU.add,
+                    out=piece, in0=acc[:, 0:n], in1=bias[:, base + off : base + off + n], op=ALU.add
                 )
-                if after is not None:
-                    nc.vector.tensor_scalar(
-                        out=dest[:, off : off + n], in0=dest[:, off : off + n],
-                        scalar1=lo, scalar2=hi, op0=ALU.max, op1=ALU.min,
-                    )
-                    after(off, n)
-            if after is None:
-                nc.vector.tensor_scalar(
-                    out=dest[:], in0=dest[:], scalar1=lo, scalar2=hi, op0=ALU.max, op1=ALU.min
-                )
+                nc.vector.tensor_scalar(out=piece, in0=piece, scalar1=lo, scalar2=hi, op0=ALU.max, op1=ALU.min)
+                after(off, n)
 
         three = [BANK, BANK, BANK]
-        acc_c = keep.tile([P, H], F32)
-        gate(COL_F, three, acc_c, -3.0, 3.0, None)
-        nc.vector.scalar_tensor_tensor(
-            out=acc_c[:], in0=acc_c[:], scalar=3.0, in1=c0_sb[:], op0=ALU.add, op1=ALU.mult
-        )
+        csum = keep.tile([P, H], F32)
         gi = keep.tile([P, H], F32)
-        gate(COL_I, three, gi, -3.0, 3.0, None)
         gg = keep.tile([P, H], F32)
-        gate(COL_G, three, gg, -1.0, 1.0, None)
-        nc.vector.scalar_tensor_tensor(
-            out=gg[:], in0=gi[:], scalar=3.0, in1=gg[:], op0=ALU.add, op1=ALU.mult
-        )
-        nc.vector.tensor_tensor(out=acc_c[:], in0=acc_c[:], in1=gg[:], op=ALU.add)
-        c1 = keep.tile([P, H], F32)
-        nc.vector.tensor_scalar(out=c1[:], in0=acc_c[:], scalar1=1.0 / 6.0, scalar2=None, op0=ALU.mult)
-        nc.scalar.dma_start(out=out_1, in_=c1[:])
         th = keep.tile([P, H], F32)
-        nc.vector.tensor_scalar(
-            out=th[:], in0=acc_c[:], scalar1=-6.0, scalar2=6.0, op0=ALU.max, op1=ALU.min
-        )
-        nc.vector.tensor_scalar(out=th[:], in0=th[:], scalar1=1.0 / 36.0, scalar2=None, op0=ALU.mult)
-
+        c1 = keep.tile([P, H], F32)
         go = keep.tile([P, H], F32)
 
-        def finish(off, n):
+        def after_f(off, n):
+            s = slice(off, off + n)
             nc.vector.scalar_tensor_tensor(
-                out=go[:, off : off + n], in0=go[:, off : off + n], scalar=3.0,
-                in1=th[:, off : off + n], op0=ALU.add, op1=ALU.mult,
+                out=csum[:, s], in0=csum[:, s], scalar=3.0, in1=c0s[:, s], op0=ALU.add, op1=ALU.mult
             )
-            nc.sync.dma_start(out=out_0[:, off : off + n], in_=go[:, off : off + n])
 
-        gate(COL_O, [BANK, BANK, 256, 256], go, -3.0, 3.0, finish)
+        def after_i(off, n):
+            s = slice(off, off + n)
+            nc.vector.tensor_scalar(
+                out=gi[:, s], in0=gi[:, s], scalar1=3.0, scalar2=1.0 / 36.0, op0=ALU.add, op1=ALU.mult
+            )
+
+        def after_g(off, n):
+            s = slice(off, off + n)
+            nc.vector.tensor_tensor(out=gg[:, s], in0=gg[:, s], in1=gi[:, s], op=ALU.mult)
+            nc.vector.tensor_tensor(out=csum[:, s], in0=csum[:, s], in1=gg[:, s], op=ALU.add)
+            nc.vector.tensor_scalar(
+                out=th[:, s], in0=csum[:, s], scalar1=-1.0 / 6.0, scalar2=1.0 / 6.0, op0=ALU.max, op1=ALU.min
+            )
+
+        def after_o(off, n):
+            s = slice(off, off + n)
+            nc.vector.scalar_tensor_tensor(
+                out=go[:, s], in0=go[:, s], scalar=3.0, in1=th[:, s], op0=ALU.add, op1=ALU.mult
+            )
+            nc.sync.dma_start(out=out_0[:, s], in_=go[:, s])
+
+        gate(COL_F, three, PASSES, csum, -3.0, 3.0, after_f)
+        gate(COL_I, three, PASSES, gi, -3.0, 3.0, after_i)
+        gate(COL_G, three, PASSES, gg, -1.0, 1.0, after_g)
+        nc.vector.tensor_scalar(out=c1[:], in0=csum[:], scalar1=6.0, scalar2=None, op0=ALU.mult)
+        gate(COL_O, [BANK, BANK, 256, 256], PASSES_IH, go, -3.0, 3.0, after_o)

@@ -20,7 +20,6 @@ PASSES_IH = IN // 512
 PASSES_HH = H // 512
 PASSES = PASSES_IH + PASSES_HH
 BANK = 512
-W_BUFS = 20
 FLOPS = 2 * B * (IN + H) * NG
 
 COL_F, COL_I, COL_O, COL_G = 0, H, 2 * H, 3 * H
@@ -32,7 +31,8 @@ def tile_qlstmcell_w_kernel(
     nc = tc.nc
     with ExitStack() as ctx:
         keep = ctx.enter_context(tc.tile_pool(name="keep", bufs=1))
-        wpool = ctx.enter_context(tc.tile_pool(name="wpool", bufs=W_BUFS))
+        wide = ctx.enter_context(tc.tile_pool(name="wide", bufs=5))
+        narrow = ctx.enter_context(tc.tile_pool(name="narrow", bufs=11))
         psum = ctx.enter_context(tc.psum_pool(name="psum", bufs=8))
 
         ident = keep.tile([P, P], F32)
@@ -89,31 +89,28 @@ def tile_qlstmcell_w_kernel(
                 in_=grouped[:, first : first + n].rearrange("p g r t -> p (g r t)"),
             )
 
-        c0s = keep.tile([P, H], F32)
-        nc.vector.tensor_scalar(out=c0s[:], in0=c0_sb[:], scalar1=1.0 / 36.0, scalar2=None, op0=ALU.mult)
-
-        bias = keep.tile([P, NG], BF16)
+        bias = keep.tile([P, NG], F32)
         for base in (COL_F, COL_I, COL_G, COL_O):
             for c in range(base, base + H, BANK):
                 pb = psum.tile([P, BANK], F32, tag="bank")
                 nc.tensor.matmul(out=pb[:], lhsT=ones[:], rhs=brow[:, c : c + BANK], start=True, stop=True)
-                nc.scalar.copy(out=bias[:, c : c + BANK], in_=pb[:])
+                if base == COL_G:
+                    nc.scalar.copy(out=bias[:, c : c + BANK], in_=pb[:])
+                else:
+                    nc.vector.tensor_scalar(
+                        out=bias[:, c : c + BANK], in0=pb[:], scalar1=1.0 / 6.0, scalar2=0.5,
+                        op0=ALU.mult, op1=ALU.add,
+                    )
 
-        def load(g, c_lo, c_hi):
-            words = W_ih_words[g] if g < PASSES_IH else W_hh_words[g - PASSES_IH]
-            wt = wpool.tile([P, H], U32, tag="w", align_bytes=64)
+        def load(pool, width, g_lo, g_hi, c_lo, c_hi):
+            src, shift = (W_ih_words, 0) if g_lo < PASSES_IH else (W_hh_words, PASSES_IH)
+            count = g_hi - g_lo
+            wt = pool.tile([P, width], U32, tag="w", align_bytes=64)
             nc.sync.dma_start(
-                out=wt[:, 0 : c_hi - c_lo].bitcast(I32),
-                in_=words.rearrange("p n t -> p (n t)")[:, 4 * c_lo : 4 * c_hi].bitcast(I32),
-            )
-            return wt
-
-        def load_hh(c_lo, c_hi):
-            n = c_hi - c_lo
-            wt = wpool.tile([P, H], U32, tag="w", align_bytes=64)
-            nc.sync.dma_start(
-                out=wt[:, 0 : PASSES_HH * n].rearrange("p (g n) -> p g n", g=PASSES_HH).bitcast(I32),
-                in_=W_hh_words.rearrange("g p n t -> p g (n t)")[:, :, 4 * c_lo : 4 * c_hi].bitcast(I32),
+                out=wt[:, 0 : count * (c_hi - c_lo)].rearrange("p (g n) -> p g n", g=count).bitcast(I32),
+                in_=src.rearrange("g p n t -> p g (n t)")[
+                    :, g_lo - shift : g_hi - shift, 4 * c_lo : 4 * c_hi
+                ].bitcast(I32),
             )
             return wt
 
@@ -130,64 +127,70 @@ def tile_qlstmcell_w_kernel(
                 stop=(g == PASSES - 1),
             )
 
-        def gate(base, widths, whole_passes, dest, lo, hi, after):
-            offs = [sum(widths[:i]) for i in range(len(widths))]
-            accs = [psum.tile([P, BANK], F32, tag="bank", name="acc") for w in widths]
-            for g in range(whole_passes):
-                wt = load(g, base, base + H)
-                for acc, off, n in zip(accs, offs, widths):
-                    mx_pass(acc, g, wt, off, base + off, n)
-            if whole_passes < PASSES:
-                for acc, off, n in zip(accs, offs, widths):
-                    part = load_hh(base + off, base + off + n)
-                    for g in range(PASSES_IH, PASSES):
-                        mx_pass(acc, g, part, (g - PASSES_IH) * n, base + off, n)
-                nc.sync.dma_start(out=out_1, in_=c1[:])
-            for acc, off, n in zip(accs, offs, widths):
-                piece = dest[:, off : off + n]
-                nc.vector.tensor_tensor(
-                    out=piece, in0=acc[:, 0:n], in1=bias[:, base + off : base + off + n], op=ALU.add
-                )
-                nc.vector.tensor_scalar(out=piece, in0=piece, scalar1=lo, scalar2=hi, op0=ALU.max, op1=ALU.min)
-                after(off, n)
+        def banks(count):
+            return [psum.tile([P, BANK], F32, tag="bank", name="acc") for j in range(count)]
 
-        three = [BANK, BANK, BANK]
-        csum = keep.tile([P, H], F32)
+        def hard_sigmoid(dest, acc, col, n):
+            nc.vector.scalar_tensor_tensor(
+                out=dest, in0=acc[:, 0:n], scalar=1.0 / 6.0, in1=bias[:, col : col + n],
+                op0=ALU.mult, op1=ALU.add,
+            )
+            nc.vector.tensor_scalar(out=dest, in0=dest, scalar1=0.0, scalar2=1.0, op0=ALU.max, op1=ALU.min)
+
+        c1 = keep.tile([P, H], F32)
         gi = keep.tile([P, H], F32)
         gg = keep.tile([P, H], F32)
         th = keep.tile([P, H], F32)
-        c1 = keep.tile([P, H], F32)
-        go = keep.tile([P, H], F32)
+        h1 = keep.tile([P, H], F32)
 
-        def after_f(off, n):
-            s = slice(off, off + n)
-            nc.vector.scalar_tensor_tensor(
-                out=csum[:, s], in0=csum[:, s], scalar=3.0, in1=c0s[:, s], op0=ALU.add, op1=ALU.mult
+        acc_fi = banks(6)
+        for g in range(PASSES):
+            wt = load(wide, 2 * H, g, g + 1, COL_F, COL_F + 2 * H)
+            for j in range(6):
+                mx_pass(acc_fi[j], g, wt, j * BANK, COL_F + j * BANK, BANK)
+        for j in range(3):
+            s = slice(j * BANK, (j + 1) * BANK)
+            hard_sigmoid(c1[:, s], acc_fi[j], COL_F + j * BANK, BANK)
+            nc.vector.tensor_tensor(out=c1[:, s], in0=c1[:, s], in1=c0_sb[:, s], op=ALU.mult)
+        for j in range(3):
+            s = slice(j * BANK, (j + 1) * BANK)
+            hard_sigmoid(gi[:, s], acc_fi[3 + j], COL_I + j * BANK, BANK)
+
+        acc_g = banks(3)
+        for g in range(PASSES):
+            wt = load(narrow, H, g, g + 1, COL_G, COL_G + H)
+            for j in range(3):
+                mx_pass(acc_g[j], g, wt, j * BANK, COL_G + j * BANK, BANK)
+        for j in range(3):
+            s = slice(j * BANK, (j + 1) * BANK)
+            nc.vector.tensor_tensor(
+                out=gg[:, s], in0=acc_g[j][:], in1=bias[:, COL_G + j * BANK : COL_G + (j + 1) * BANK], op=ALU.add
             )
-
-        def after_i(off, n):
-            s = slice(off, off + n)
-            nc.vector.tensor_scalar(
-                out=gi[:, s], in0=gi[:, s], scalar1=3.0, scalar2=1.0 / 36.0, op0=ALU.add, op1=ALU.mult
-            )
-
-        def after_g(off, n):
-            s = slice(off, off + n)
+            nc.vector.tensor_scalar(out=gg[:, s], in0=gg[:, s], scalar1=-1.0, scalar2=1.0, op0=ALU.max, op1=ALU.min)
             nc.vector.tensor_tensor(out=gg[:, s], in0=gg[:, s], in1=gi[:, s], op=ALU.mult)
-            nc.vector.tensor_tensor(out=csum[:, s], in0=csum[:, s], in1=gg[:, s], op=ALU.add)
-            nc.vector.tensor_scalar(
-                out=th[:, s], in0=csum[:, s], scalar1=-1.0 / 6.0, scalar2=1.0 / 6.0, op0=ALU.max, op1=ALU.min
-            )
+            nc.vector.tensor_tensor(out=c1[:, s], in0=c1[:, s], in1=gg[:, s], op=ALU.add)
+            nc.vector.tensor_scalar(out=th[:, s], in0=c1[:, s], scalar1=-1.0, scalar2=1.0, op0=ALU.max, op1=ALU.min)
 
-        def after_o(off, n):
+        acc_o = banks(4)
+        pieces = [(0, BANK), (BANK, BANK), (2 * BANK, 256), (2 * BANK + 256, 256)]
+        for g in range(PASSES):
+            wt = load(narrow, H, g, g + 1, COL_O, COL_O + 2 * BANK)
+            for j in range(2):
+                mx_pass(acc_o[j], g, wt, j * BANK, COL_O + j * BANK, BANK)
+        wt = load(wide, 2 * H, 0, PASSES_IH, COL_O + 2 * BANK, COL_O + H)
+        for g in range(PASSES_IH):
+            for j in (2, 3):
+                off, n = pieces[j]
+                mx_pass(acc_o[j], g, wt, g * BANK + off - 2 * BANK, COL_O + off, n)
+        for j in (2, 3):
+            off, n = pieces[j]
+            wt = load(narrow, H, PASSES_IH, PASSES, COL_O + off, COL_O + off + n)
+            for g in range(PASSES_IH, PASSES):
+                mx_pass(acc_o[j], g, wt, (g - PASSES_IH) * n, COL_O + off, n)
+        nc.sync.dma_start(out=out_1, in_=c1[:])
+        for j in range(4):
+            off, n = pieces[j]
             s = slice(off, off + n)
-            nc.vector.scalar_tensor_tensor(
-                out=go[:, s], in0=go[:, s], scalar=3.0, in1=th[:, s], op0=ALU.add, op1=ALU.mult
-            )
-            nc.sync.dma_start(out=out_0[:, s], in_=go[:, s])
-
-        gate(COL_F, three, PASSES, csum, -3.0, 3.0, after_f)
-        gate(COL_I, three, PASSES, gi, -3.0, 3.0, after_i)
-        gate(COL_G, three, PASSES, gg, -1.0, 1.0, after_g)
-        nc.vector.tensor_scalar(out=c1[:], in0=csum[:], scalar1=6.0, scalar2=None, op0=ALU.mult)
-        gate(COL_O, [BANK, BANK, 256, 256], PASSES_IH, go, -3.0, 3.0, after_o)
+            hard_sigmoid(h1[:, s], acc_o[j], COL_O + off, n)
+            nc.vector.tensor_tensor(out=h1[:, s], in0=h1[:, s], in1=th[:, s], op=ALU.mult)
+            nc.sync.dma_start(out=out_0[:, s], in_=h1[:, s])

@@ -130,18 +130,23 @@ def tile_qlstmcell_w_kernel(
         def banks(count):
             return [psum.tile([P, BANK], F32, tag="bank", name="acc") for j in range(count)]
 
-        def hard_sigmoid(dest, acc, col, n):
+        def gate_line(dest, acc, col, n):
             nc.vector.scalar_tensor_tensor(
                 out=dest, in0=acc[:, 0:n], scalar=1.0 / 6.0, in1=bias[:, col : col + n],
                 op0=ALU.mult, op1=ALU.add,
             )
-            nc.vector.tensor_scalar(out=dest, in0=dest, scalar1=0.0, scalar2=1.0, op0=ALU.max, op1=ALU.min)
+
+        def clip(dest, src, low, high):
+            nc.vector.tensor_scalar(out=dest, in0=src, scalar1=low, scalar2=high, op0=ALU.max, op1=ALU.min)
 
         c1 = keep.tile([P, H], F32)
         gi = keep.tile([P, H], F32)
         gg = keep.tile([P, H], F32)
         th = keep.tile([P, H], F32)
         h1 = keep.tile([P, H], F32)
+        cols = [slice(j * BANK, (j + 1) * BANK) for j in range(3)]
+
+        ctx.enter_context(tc.manual_schedule(engines={mybir.EngineType.DVE}))
 
         acc_fi = banks(6)
         for g in range(PASSES):
@@ -149,12 +154,15 @@ def tile_qlstmcell_w_kernel(
             for j in range(6):
                 mx_pass(acc_fi[j], g, wt, j * BANK, COL_F + j * BANK, BANK)
         for j in range(3):
-            s = slice(j * BANK, (j + 1) * BANK)
-            hard_sigmoid(c1[:, s], acc_fi[j], COL_F + j * BANK, BANK)
-            nc.vector.tensor_tensor(out=c1[:, s], in0=c1[:, s], in1=c0_sb[:, s], op=ALU.mult)
+            gate_line(c1[:, cols[j]], acc_fi[j], COL_F + j * BANK, BANK)
         for j in range(3):
-            s = slice(j * BANK, (j + 1) * BANK)
-            hard_sigmoid(gi[:, s], acc_fi[3 + j], COL_I + j * BANK, BANK)
+            gate_line(gi[:, cols[j]], acc_fi[3 + j], COL_I + j * BANK, BANK)
+        for j in range(3):
+            clip(c1[:, cols[j]], c1[:, cols[j]], 0.0, 1.0)
+        for j in range(3):
+            clip(gi[:, cols[j]], gi[:, cols[j]], 0.0, 1.0)
+        for j in range(3):
+            nc.vector.tensor_tensor(out=c1[:, cols[j]], in0=c1[:, cols[j]], in1=c0_sb[:, cols[j]], op=ALU.mult)
 
         acc_g = banks(3)
         for g in range(PASSES):
@@ -162,14 +170,17 @@ def tile_qlstmcell_w_kernel(
             for j in range(3):
                 mx_pass(acc_g[j], g, wt, j * BANK, COL_G + j * BANK, BANK)
         for j in range(3):
-            s = slice(j * BANK, (j + 1) * BANK)
             nc.vector.tensor_tensor(
-                out=gg[:, s], in0=acc_g[j][:], in1=bias[:, COL_G + j * BANK : COL_G + (j + 1) * BANK], op=ALU.add
+                out=gg[:, cols[j]], in0=acc_g[j][:], in1=bias[:, COL_G + j * BANK : COL_G + (j + 1) * BANK], op=ALU.add
             )
-            nc.vector.tensor_scalar(out=gg[:, s], in0=gg[:, s], scalar1=-1.0, scalar2=1.0, op0=ALU.max, op1=ALU.min)
-            nc.vector.tensor_tensor(out=gg[:, s], in0=gg[:, s], in1=gi[:, s], op=ALU.mult)
-            nc.vector.tensor_tensor(out=c1[:, s], in0=c1[:, s], in1=gg[:, s], op=ALU.add)
-            nc.vector.tensor_scalar(out=th[:, s], in0=c1[:, s], scalar1=-1.0, scalar2=1.0, op0=ALU.max, op1=ALU.min)
+        for j in range(3):
+            clip(gg[:, cols[j]], gg[:, cols[j]], -1.0, 1.0)
+        for j in range(3):
+            nc.vector.tensor_tensor(out=gg[:, cols[j]], in0=gg[:, cols[j]], in1=gi[:, cols[j]], op=ALU.mult)
+        for j in range(3):
+            nc.vector.tensor_tensor(out=c1[:, cols[j]], in0=c1[:, cols[j]], in1=gg[:, cols[j]], op=ALU.add)
+        for j in range(3):
+            clip(th[:, cols[j]], c1[:, cols[j]], -1.0, 1.0)
 
         acc_o = banks(4)
         pieces = [(0, BANK), (BANK, BANK), (2 * BANK, 256), (2 * BANK + 256, 256)]
@@ -188,9 +199,17 @@ def tile_qlstmcell_w_kernel(
             for g in range(PASSES_IH, PASSES):
                 mx_pass(acc_o[j], g, wt, (g - PASSES_IH) * n, COL_O + off, n)
         nc.sync.dma_start(out=out_1, in_=c1[:])
-        for j in range(4):
+
+        def o_step(step, j):
             off, n = pieces[j]
             s = slice(off, off + n)
-            hard_sigmoid(h1[:, s], acc_o[j], COL_O + off, n)
-            nc.vector.tensor_tensor(out=h1[:, s], in0=h1[:, s], in1=th[:, s], op=ALU.mult)
-            nc.sync.dma_start(out=out_0[:, s], in_=h1[:, s])
+            if step == 0:
+                gate_line(h1[:, s], acc_o[j], COL_O + off, n)
+            elif step == 1:
+                clip(h1[:, s], h1[:, s], 0.0, 1.0)
+            else:
+                nc.vector.tensor_tensor(out=h1[:, s], in0=h1[:, s], in1=th[:, s], op=ALU.mult)
+                nc.sync.dma_start(out=out_0[:, s], in_=h1[:, s])
+
+        for step, j in ((0, 0), (0, 1), (1, 0), (1, 1), (2, 0), (2, 1), (0, 2), (1, 2), (0, 3), (2, 2), (1, 3), (2, 3)):
+            o_step(step, j)

@@ -62,9 +62,9 @@ def tile_qlstmcell_w_kernel(
         nc.vector.memset(brow[:].bitcast(I32), 0)
         ones = keep.tile([P, P], BF16)
         nc.vector.memset(ones[:], 1.0)
-        nc.scalar.dma_start(out=brow[0:1, :], in_=b_hh.rearrange("(o n) -> o n", o=1))
+        nc.sync.dma_start(out=brow[0:1, :], in_=b_hh.rearrange("(o n) -> o n", o=1))
         c0_sb = keep.tile([P, H], BF16)
-        nc.scalar.dma_start(out=c0_sb[:], in_=c_0)
+        nc.sync.dma_start(out=c0_sb[:], in_=c_0)
 
         xh_words = xh[:].bitcast(F32)
         grouped = keep.tile([P, PASSES, B, 4], BF16, align_bytes=64)

@@ -35,6 +35,8 @@ def tile_qlstmcell_w_kernel(
         narrow = ctx.enter_context(tc.tile_pool(name="narrow", bufs=11))
         psum = ctx.enter_context(tc.psum_pool(name="psum", bufs=8))
 
+        ctx.enter_context(tc.manual_schedule(engines={mybir.EngineType.SP, mybir.EngineType.DVE}))
+
         ident = keep.tile([P, P], F32)
         make_identity(nc, ident[:])
 
@@ -47,15 +49,28 @@ def tile_qlstmcell_w_kernel(
         nc.sync.dma_start(out=xh[:, 0:IN], in_=input_)
         nc.sync.dma_start(out=xh[:, IN : IN + H], in_=h_0)
 
+        def load(pool, width, g_lo, g_hi, c_lo, c_hi):
+            src, shift = (W_ih_words, 0) if g_lo < PASSES_IH else (W_hh_words, PASSES_IH)
+            count = g_hi - g_lo
+            wt = pool.tile([P, width], U32, tag="w", align_bytes=64)
+            nc.sync.dma_start(
+                out=wt[:, 0 : count * (c_hi - c_lo)].rearrange("p (g n) -> p g n", g=count).bitcast(I32),
+                in_=src.rearrange("g p n t -> p g (n t)")[
+                    :, g_lo - shift : g_hi - shift, 4 * c_lo : 4 * c_hi
+                ].bitcast(I32),
+            )
+            return wt
+
+        first_fi = load(wide, 2 * H, 0, 1, COL_F, COL_F + 2 * H)
         for q in range(4):
-            nc.gpsimd.dma_start(
-                out=planes_ih[32 * q : 32 * q + 16, :].bitcast(F32),
-                in_=W_ih_scales[:, 4 * q : 4 * q + 4, :].bitcast(F32),
+            nc.sync.dma_start(
+                out=planes_ih[32 * q : 32 * q + 16, :].bitcast(I32),
+                in_=W_ih_scales[:, 4 * q : 4 * q + 4, :].bitcast(I32),
             )
         for q in range(4):
-            nc.gpsimd.dma_start(
-                out=planes_hh[32 * q : 32 * q + 12, :].bitcast(F32),
-                in_=W_hh_scales[:, 4 * q : 4 * q + 4, :].bitcast(F32),
+            nc.sync.dma_start(
+                out=planes_hh[32 * q : 32 * q + 12, :].bitcast(I32),
+                in_=W_hh_scales[:, 4 * q : 4 * q + 4, :].bitcast(I32),
             )
 
         brow = keep.tile([P, NG], BF16)
@@ -102,18 +117,6 @@ def tile_qlstmcell_w_kernel(
                         op0=ALU.mult, op1=ALU.add,
                     )
 
-        def load(pool, width, g_lo, g_hi, c_lo, c_hi):
-            src, shift = (W_ih_words, 0) if g_lo < PASSES_IH else (W_hh_words, PASSES_IH)
-            count = g_hi - g_lo
-            wt = pool.tile([P, width], U32, tag="w", align_bytes=64)
-            nc.sync.dma_start(
-                out=wt[:, 0 : count * (c_hi - c_lo)].rearrange("p (g n) -> p g n", g=count).bitcast(I32),
-                in_=src.rearrange("g p n t -> p g (n t)")[
-                    :, g_lo - shift : g_hi - shift, 4 * c_lo : 4 * c_hi
-                ].bitcast(I32),
-            )
-            return wt
-
         def mx_pass(acc, g, wt, off, col, n):
             planes = planes_ih if g < PASSES_IH else planes_hh
             k = 4 * (g % PASSES_IH)
@@ -146,11 +149,10 @@ def tile_qlstmcell_w_kernel(
         h1 = keep.tile([P, H], F32)
         cols = [slice(j * BANK, (j + 1) * BANK) for j in range(3)]
 
-        ctx.enter_context(tc.manual_schedule(engines={mybir.EngineType.DVE}))
 
         acc_fi = banks(6)
         for g in range(PASSES):
-            wt = load(wide, 2 * H, g, g + 1, COL_F, COL_F + 2 * H)
+            wt = first_fi if g == 0 else load(wide, 2 * H, g, g + 1, COL_F, COL_F + 2 * H)
             for j in range(6):
                 mx_pass(acc_fi[j], g, wt, j * BANK, COL_F + j * BANK, BANK)
         for j in range(3):

@@ -47,12 +47,14 @@ def tile_qlstmcell_w_kernel(
 
         xh = keep.tile([P, IN + H], BF16, align_bytes=64)
         nc.sync.dma_start(out=xh[:, 0:IN], in_=input_)
-        nc.sync.dma_start(out=xh[:, IN : IN + H], in_=h_0)
 
-        def load(pool, width, g_lo, g_hi, c_lo, c_hi):
+        def load(pool, width, g_lo, g_hi, c_lo, c_hi, behind_scales=False):
             src, shift = (W_ih_words, 0) if g_lo < PASSES_IH else (W_hh_words, PASSES_IH)
             count = g_hi - g_lo
             wt = pool.tile([P, width], U32, tag="w", align_bytes=64)
+            if behind_scales:
+                nc.vector.tensor_copy(out=wt[:, 0:1].bitcast(U8), in_=planes_ih[:, 0:4])
+                nc.vector.tensor_copy(out=wt[:, 1:2].bitcast(U8), in_=planes_hh[:, 0:4])
             nc.sync.dma_start(
                 out=wt[:, 0 : count * (c_hi - c_lo)].rearrange("p (g n) -> p g n", g=count).bitcast(I32),
                 in_=src.rearrange("g p n t -> p g (n t)")[
@@ -61,7 +63,6 @@ def tile_qlstmcell_w_kernel(
             )
             return wt
 
-        first_fi = load(wide, 2 * H, 0, 1, COL_F, COL_F + 2 * H)
         for q in range(4):
             nc.sync.dma_start(
                 out=planes_ih[32 * q : 32 * q + 16, :].bitcast(I32),
@@ -72,6 +73,7 @@ def tile_qlstmcell_w_kernel(
                 out=planes_hh[32 * q : 32 * q + 12, :].bitcast(I32),
                 in_=W_hh_scales[:, 4 * q : 4 * q + 4, :].bitcast(I32),
             )
+        nc.sync.dma_start(out=xh[:, IN : IN + H], in_=h_0)
 
         brow = keep.tile([P, NG], BF16)
         nc.vector.memset(brow[:].bitcast(I32), 0)
@@ -103,6 +105,8 @@ def tile_qlstmcell_w_kernel(
                 scales=xs[:, first : first + n, :].rearrange("p g r -> p (g r)"),
                 in_=grouped[:, first : first + n].rearrange("p g r t -> p (g r t)"),
             )
+            if first + n == PASSES_IH:
+                first_fi = load(wide, 2 * H, 0, 1, COL_F, COL_F + 2 * H, behind_scales=True)
 
         bias = keep.tile([P, NG], F32)
         for base in (COL_F, COL_I, COL_G, COL_O):

@@ -44,6 +44,10 @@ def tile_qlstmcell_w_kernel(
         planes_hh = keep.tile([P, NG], U8, align_bytes=64)
         nc.vector.memset(planes_ih[:].bitcast(I32), 0)
         nc.vector.memset(planes_hh[:].bitcast(I32), 0)
+        brow = keep.tile([P, NG], BF16)
+        nc.vector.memset(brow[:].bitcast(I32), 0)
+        ones = keep.tile([P, P], BF16)
+        nc.vector.memset(ones[:], 1.0)
 
         xh = keep.tile([P, IN + H], BF16, align_bytes=64)
         nc.sync.dma_start(out=xh[:, 0:IN], in_=input_)
@@ -53,8 +57,7 @@ def tile_qlstmcell_w_kernel(
             count = g_hi - g_lo
             wt = pool.tile([P, width], U32, tag="w", align_bytes=64)
             if behind_scales:
-                nc.vector.tensor_copy(out=wt[:, 0:1].bitcast(U8), in_=planes_ih[:, 0:4])
-                nc.vector.tensor_copy(out=wt[:, 1:2].bitcast(U8), in_=planes_hh[:, 0:4])
+                nc.vector.tensor_copy(out=wt[64:96, 0:1].bitcast(I32), in_=planes_ih[64:96, 0:4].bitcast(I32))
             nc.sync.dma_start(
                 out=wt[:, 0 : count * (c_hi - c_lo)].rearrange("p (g n) -> p g n", g=count).bitcast(I32),
                 in_=src.rearrange("g p n t -> p g (n t)")[
@@ -63,22 +66,16 @@ def tile_qlstmcell_w_kernel(
             )
             return wt
 
-        for q in range(4):
-            nc.sync.dma_start(
-                out=planes_ih[32 * q : 32 * q + 16, :].bitcast(I32),
-                in_=W_ih_scales[:, 4 * q : 4 * q + 4, :].bitcast(I32),
-            )
-        for q in range(4):
-            nc.sync.dma_start(
-                out=planes_hh[32 * q : 32 * q + 12, :].bitcast(I32),
-                in_=W_hh_scales[:, 4 * q : 4 * q + 4, :].bitcast(I32),
-            )
+        for half in ((2, 3), (0, 1)):
+            for planes, scales, rows in ((planes_ih, W_ih_scales, 16), (planes_hh, W_hh_scales, 12)):
+                for q in half:
+                    nc.sync.dma_start(
+                        out=planes[32 * q : 32 * q + rows, :].bitcast(I32),
+                        in_=scales[:, 4 * q : 4 * q + 4, :].bitcast(I32),
+                    )
+        first_fi = load(wide, 2 * H, 0, 1, COL_F, COL_F + 2 * H, behind_scales=True)
         nc.sync.dma_start(out=xh[:, IN : IN + H], in_=h_0)
 
-        brow = keep.tile([P, NG], BF16)
-        nc.vector.memset(brow[:].bitcast(I32), 0)
-        ones = keep.tile([P, P], BF16)
-        nc.vector.memset(ones[:], 1.0)
         nc.sync.dma_start(out=brow[0:1, :], in_=b_hh.rearrange("(o n) -> o n", o=1))
         c0_sb = keep.tile([P, H], BF16)
         nc.sync.dma_start(out=c0_sb[:], in_=c_0)
@@ -105,8 +102,6 @@ def tile_qlstmcell_w_kernel(
                 scales=xs[:, first : first + n, :].rearrange("p g r -> p (g r)"),
                 in_=grouped[:, first : first + n].rearrange("p g r t -> p (g r t)"),
             )
-            if first + n == PASSES_IH:
-                first_fi = load(wide, 2 * H, 0, 1, COL_F, COL_F + 2 * H, behind_scales=True)
 
         bias = keep.tile([P, NG], F32)
         for base in (COL_F, COL_I, COL_G, COL_O):

@@ -10,6 +10,7 @@ U32 = mybir.dt.uint32
 U8 = mybir.dt.uint8
 FP8X4 = mybir.dt.float8_e4m3fn_x4
 ALU = mybir.AluOpType
+ACT = mybir.ActivationFunctionType
 
 P = 128
 B = 128
@@ -31,11 +32,11 @@ def tile_qlstmcell_w_kernel(
     nc = tc.nc
     with ExitStack() as ctx:
         keep = ctx.enter_context(tc.tile_pool(name="keep", bufs=1))
-        wide = ctx.enter_context(tc.tile_pool(name="wide", bufs=5))
-        narrow = ctx.enter_context(tc.tile_pool(name="narrow", bufs=11))
         psum = ctx.enter_context(tc.psum_pool(name="psum", bufs=8))
 
-        ctx.enter_context(tc.manual_schedule(engines={mybir.EngineType.SP, mybir.EngineType.DVE}))
+        ctx.enter_context(
+            tc.manual_schedule(engines={mybir.EngineType.SP, mybir.EngineType.DVE, mybir.EngineType.PE})
+        )
 
         ident = keep.tile([P, P], F32)
         make_identity(nc, ident[:])
@@ -44,27 +45,22 @@ def tile_qlstmcell_w_kernel(
         planes_hh = keep.tile([P, NG], U8, align_bytes=64)
         nc.vector.memset(planes_ih[:].bitcast(I32), 0)
         nc.vector.memset(planes_hh[:].bitcast(I32), 0)
-        brow = keep.tile([P, NG], BF16)
-        nc.vector.memset(brow[:].bitcast(I32), 0)
+        bias = keep.tile([P, NG], BF16)
+        nc.vector.memset(bias[:].bitcast(I32), 0)
         ones = keep.tile([P, P], BF16)
         nc.vector.memset(ones[:], 1.0)
 
-        xh = keep.tile([P, IN + H], BF16, align_bytes=64)
+        xh = keep.tile([P, IN + H], BF16, align_bytes=64, tag="x_then_g")
         nc.sync.dma_start(out=xh[:, 0:IN], in_=input_)
 
-        def load(pool, width, g_lo, g_hi, c_lo, c_hi, behind_scales=False):
-            src, shift = (W_ih_words, 0) if g_lo < PASSES_IH else (W_hh_words, PASSES_IH)
-            count = g_hi - g_lo
-            wt = pool.tile([P, width], U32, tag="w", align_bytes=64)
-            if behind_scales:
-                nc.vector.tensor_copy(out=wt[64:96, 0:1].bitcast(I32), in_=planes_ih[64:96, 0:4].bitcast(I32))
+        words = [keep.tile([P, NG], U32, align_bytes=64, name="words%d" % g) for g in range(PASSES)]
+
+        def load(g, lo, hi):
+            src, k = (W_ih_words, g) if g < PASSES_IH else (W_hh_words, g - PASSES_IH)
             nc.sync.dma_start(
-                out=wt[:, 0 : count * (c_hi - c_lo)].rearrange("p (g n) -> p g n", g=count).bitcast(I32),
-                in_=src.rearrange("g p n t -> p g (n t)")[
-                    :, g_lo - shift : g_hi - shift, 4 * c_lo : 4 * c_hi
-                ].bitcast(I32),
+                out=words[g][:, lo:hi].bitcast(I32),
+                in_=src.rearrange("g p n t -> g p (n t)")[k, :, 4 * lo : 4 * hi].bitcast(I32),
             )
-            return wt
 
         for half in ((2, 3), (0, 1)):
             for planes, scales, rows in ((planes_ih, W_ih_scales, 16), (planes_hh, W_hh_scales, 12)):
@@ -73,15 +69,27 @@ def tile_qlstmcell_w_kernel(
                         out=planes[32 * q : 32 * q + rows, :].bitcast(I32),
                         in_=scales[:, 4 * q : 4 * q + 4, :].bitcast(I32),
                     )
-        first_fi = load(wide, 2 * H, 0, 1, COL_F, COL_F + 2 * H, behind_scales=True)
+        nc.vector.tensor_copy(out=words[0][64:96, 0:1].bitcast(I32), in_=planes_ih[64:96, 0:4].bitcast(I32))
+        load(0, 0, NG)
         nc.sync.dma_start(out=xh[:, IN : IN + H], in_=h_0)
-
-        nc.sync.dma_start(out=brow[0:1, :], in_=b_hh.rearrange("(o n) -> o n", o=1))
+        nc.sync.dma_start(out=bias[0:1, :], in_=b_hh.rearrange("(o n) -> o n", o=1))
         c0_sb = keep.tile([P, H], BF16)
         nc.sync.dma_start(out=c0_sb[:], in_=c_0)
+        for g in range(1, PASSES_IH):
+            load(g, 0, NG)
+        for g in range(PASSES_IH, PASSES):
+            load(g, COL_F, COL_F + 2 * H)
+        for g in range(PASSES_IH, PASSES - 1):
+            load(g, COL_O, COL_O + 2 * H)
+        pieces = [(0, BANK), (BANK, BANK), (2 * BANK, 256), (2 * BANK + 256, 256)]
+        last = PASSES - 1
+        load(last, COL_G, COL_G + H)
+        load(last, COL_O, COL_O + 2 * BANK)
+        for off, n in pieces[2:]:
+            load(last, COL_O + off, COL_O + off + n)
 
         xh_words = xh[:].bitcast(F32)
-        grouped = keep.tile([P, PASSES, B, 4], BF16, align_bytes=64)
+        grouped = keep.tile([P, PASSES, B, 4], BF16, align_bytes=64, tag="grouped_then_th")
         xq = keep.tile([P, PASSES, B], U32, align_bytes=64)
         xs = keep.tile([P, PASSES, B], U8, align_bytes=64)
         for first in range(0, PASSES, 2):
@@ -103,114 +111,106 @@ def tile_qlstmcell_w_kernel(
                 in_=grouped[:, first : first + n].rearrange("p g r t -> p (g r t)"),
             )
 
-        bias = keep.tile([P, NG], F32)
-        for base in (COL_F, COL_I, COL_G, COL_O):
-            for c in range(base, base + H, BANK):
-                pb = psum.tile([P, BANK], F32, tag="bank")
-                nc.tensor.matmul(out=pb[:], lhsT=ones[:], rhs=brow[:, c : c + BANK], start=True, stop=True)
-                if base == COL_G:
-                    nc.scalar.copy(out=bias[:, c : c + BANK], in_=pb[:])
-                else:
-                    nc.vector.tensor_scalar(
-                        out=bias[:, c : c + BANK], in0=pb[:], scalar1=1.0 / 6.0, scalar2=0.5,
-                        op0=ALU.mult, op1=ALU.add,
-                    )
+        for c in range(0, NG, BANK):
+            pb = psum.tile([P, BANK], F32, tag="bank")
+            nc.tensor.matmul(out=pb[:], lhsT=ones[:], rhs=bias[:, c : c + BANK], start=True, stop=True)
+            nc.scalar.copy(out=bias[:, c : c + BANK], in_=pb[:])
 
-        def mx_pass(acc, g, wt, off, col, n):
+        def mx_pass(acc, g, col, n):
             planes = planes_ih if g < PASSES_IH else planes_hh
             k = 4 * (g % PASSES_IH)
             nc.tensor.matmul_mx(
                 out=acc[:, 0:n],
                 lhsT=xq[:, g, :].bitcast(FP8X4),
                 lhsT_scale=xs[:, g, :],
-                rhs=wt[:, off : off + n].bitcast(FP8X4),
+                rhs=words[g][:, col : col + n].bitcast(FP8X4),
                 rhs_scale=planes[k:P, col : col + n],
                 start=(g == 0),
                 stop=(g == PASSES - 1),
             )
 
-        def banks(count):
-            return [psum.tile([P, BANK], F32, tag="bank", name="acc") for j in range(count)]
+        def bank():
+            return psum.tile([P, BANK], F32, tag="bank", name="acc")
 
-        def gate_line(dest, acc, col, n):
-            nc.vector.scalar_tensor_tensor(
-                out=dest, in0=acc[:, 0:n], scalar=1.0 / 6.0, in1=bias[:, col : col + n],
-                op0=ALU.mult, op1=ALU.add,
-            )
+        def add_bias(dest, acc, col, n):
+            nc.vector.tensor_tensor(out=dest, in0=acc[:, 0:n], in1=bias[:, col : col + n], op=ALU.add)
 
         def clip(dest, src, low, high):
             nc.vector.tensor_scalar(out=dest, in0=src, scalar1=low, scalar2=high, op0=ALU.max, op1=ALU.min)
 
-        c1 = keep.tile([P, H], F32)
-        gi = keep.tile([P, H], F32)
-        gg = keep.tile([P, H], F32)
-        th = keep.tile([P, H], F32)
-        h1 = keep.tile([P, H], F32)
+        def plus_3_times(dest, gate, other):
+            nc.vector.scalar_tensor_tensor(out=dest, in0=gate, scalar=3.0, in1=other, op0=ALU.add, op1=ALU.mult)
+
+        six_c1 = keep.tile([P, H], F32)
+        gate = keep.tile([P, H], F32)
         cols = [slice(j * BANK, (j + 1) * BANK) for j in range(3)]
 
-
-        acc_fi = banks(6)
-        for g in range(PASSES):
-            wt = first_fi if g == 0 else load(wide, 2 * H, g, g + 1, COL_F, COL_F + 2 * H)
+        acc_fi = [bank() for j in range(6)]
+        acc_g = [bank() for j in range(2)]
+        for g in range(PASSES_IH):
             for j in range(6):
-                mx_pass(acc_fi[j], g, wt, j * BANK, COL_F + j * BANK, BANK)
+                mx_pass(acc_fi[j], g, COL_F + j * BANK, BANK)
+            for j in range(2):
+                mx_pass(acc_g[j], g, COL_G + j * BANK, BANK)
+        for g in range(PASSES_IH, PASSES):
+            for j in range(6):
+                mx_pass(acc_fi[j], g, COL_F + j * BANK, BANK)
         for j in range(3):
-            gate_line(c1[:, cols[j]], acc_fi[j], COL_F + j * BANK, BANK)
+            add_bias(six_c1[:, cols[j]], acc_fi[j], COL_F + j * BANK, BANK)
         for j in range(3):
-            gate_line(gi[:, cols[j]], acc_fi[3 + j], COL_I + j * BANK, BANK)
+            add_bias(gate[:, cols[j]], acc_fi[3 + j], COL_I + j * BANK, BANK)
         for j in range(3):
-            clip(c1[:, cols[j]], c1[:, cols[j]], 0.0, 1.0)
+            clip(six_c1[:, cols[j]], six_c1[:, cols[j]], -3.0, 3.0)
         for j in range(3):
-            clip(gi[:, cols[j]], gi[:, cols[j]], 0.0, 1.0)
+            clip(gate[:, cols[j]], gate[:, cols[j]], -3.0, 3.0)
         for j in range(3):
-            nc.vector.tensor_tensor(out=c1[:, cols[j]], in0=c1[:, cols[j]], in1=c0_sb[:, cols[j]], op=ALU.mult)
+            plus_3_times(six_c1[:, cols[j]], six_c1[:, cols[j]], c0_sb[:, cols[j]])
 
-        acc_g = banks(3)
-        for g in range(PASSES):
-            wt = load(narrow, H, g, g + 1, COL_G, COL_G + H)
+        acc_g.append(bank())
+        for g in range(PASSES_IH):
+            mx_pass(acc_g[2], g, COL_G + 2 * BANK, BANK)
+        acc_o = []
+        for off, n in pieces:
+            acc_o.append(bank())
+            for g in range(PASSES_IH):
+                mx_pass(acc_o[-1], g, COL_O + off, n)
+        for g in range(PASSES_IH, PASSES):
             for j in range(3):
-                mx_pass(acc_g[j], g, wt, j * BANK, COL_G + j * BANK, BANK)
+                mx_pass(acc_g[j], g, COL_G + j * BANK, BANK)
+            for j in range(4):
+                mx_pass(acc_o[j], g, COL_O + pieces[j][0], pieces[j][1])
+
+        gg = keep.tile([P, H], F32, align_bytes=64, tag="x_then_g")
+        th = keep.tile([P, H], F32, align_bytes=64, tag="grouped_then_th")
+        c1 = keep.tile([P, H], F32)
         for j in range(3):
-            nc.vector.tensor_tensor(
-                out=gg[:, cols[j]], in0=acc_g[j][:], in1=bias[:, COL_G + j * BANK : COL_G + (j + 1) * BANK], op=ALU.add
-            )
+            add_bias(gg[:, cols[j]], acc_g[j], COL_G + j * BANK, BANK)
         for j in range(3):
             clip(gg[:, cols[j]], gg[:, cols[j]], -1.0, 1.0)
         for j in range(3):
-            nc.vector.tensor_tensor(out=gg[:, cols[j]], in0=gg[:, cols[j]], in1=gi[:, cols[j]], op=ALU.mult)
+            plus_3_times(gg[:, cols[j]], gate[:, cols[j]], gg[:, cols[j]])
         for j in range(3):
-            nc.vector.tensor_tensor(out=c1[:, cols[j]], in0=c1[:, cols[j]], in1=gg[:, cols[j]], op=ALU.add)
+            nc.vector.tensor_tensor(
+                out=six_c1[:, cols[j]], in0=six_c1[:, cols[j]], in1=gg[:, cols[j]], op=ALU.add
+            )
         for j in range(3):
-            clip(th[:, cols[j]], c1[:, cols[j]], -1.0, 1.0)
-
-        acc_o = banks(4)
-        pieces = [(0, BANK), (BANK, BANK), (2 * BANK, 256), (2 * BANK + 256, 256)]
-        for g in range(PASSES):
-            wt = load(narrow, H, g, g + 1, COL_O, COL_O + 2 * BANK)
-            for j in range(2):
-                mx_pass(acc_o[j], g, wt, j * BANK, COL_O + j * BANK, BANK)
-        wt = load(wide, 2 * H, 0, PASSES_IH, COL_O + 2 * BANK, COL_O + H)
-        for g in range(PASSES_IH):
-            for j in (2, 3):
-                off, n = pieces[j]
-                mx_pass(acc_o[j], g, wt, g * BANK + off - 2 * BANK, COL_O + off, n)
-        for j in (2, 3):
-            off, n = pieces[j]
-            wt = load(narrow, H, PASSES_IH, PASSES, COL_O + off, COL_O + off + n)
-            for g in range(PASSES_IH, PASSES):
-                mx_pass(acc_o[j], g, wt, (g - PASSES_IH) * n, COL_O + off, n)
+            nc.scalar.activation(out=c1[:, cols[j]], in_=six_c1[:, cols[j]], func=ACT.Copy, scale=1.0 / 6.0)
+        for j in range(3):
+            clip(th[:, cols[j]], six_c1[:, cols[j]], -6.0, 6.0)
+        for j in range(3):
+            nc.scalar.activation(out=th[:, cols[j]], in_=th[:, cols[j]], func=ACT.Copy, scale=1.0 / 36.0)
         nc.sync.dma_start(out=out_1, in_=c1[:])
 
         def o_step(step, j):
             off, n = pieces[j]
             s = slice(off, off + n)
             if step == 0:
-                gate_line(h1[:, s], acc_o[j], COL_O + off, n)
+                add_bias(gate[:, s], acc_o[j], COL_O + off, n)
             elif step == 1:
-                clip(h1[:, s], h1[:, s], 0.0, 1.0)
+                clip(gate[:, s], gate[:, s], -3.0, 3.0)
             else:
-                nc.vector.tensor_tensor(out=h1[:, s], in0=h1[:, s], in1=th[:, s], op=ALU.mult)
-                nc.sync.dma_start(out=out_0[:, s], in_=h1[:, s])
+                plus_3_times(gate[:, s], gate[:, s], th[:, s])
+                nc.sync.dma_start(out=out_0[:, s], in_=gate[:, s])
 
         for step, j in ((0, 0), (0, 1), (1, 0), (1, 1), (2, 0), (2, 1), (0, 2), (1, 2), (0, 3), (2, 2), (1, 3), (2, 3)):
             o_step(step, j)

@@ -35,7 +35,14 @@ def tile_qlstmcell_w_kernel(
         psum = ctx.enter_context(tc.psum_pool(name="psum", bufs=8))
 
         ctx.enter_context(
-            tc.manual_schedule(engines={mybir.EngineType.SP, mybir.EngineType.DVE, mybir.EngineType.PE})
+            tc.manual_schedule(
+                engines={
+                    mybir.EngineType.SP,
+                    mybir.EngineType.DVE,
+                    mybir.EngineType.PE,
+                    mybir.EngineType.Activation,
+                }
+            )
         )
 
         ident = keep.tile([P, P], F32)
@@ -53,13 +60,13 @@ def tile_qlstmcell_w_kernel(
         xh = keep.tile([P, IN + H], BF16, align_bytes=64, tag="x_then_g")
         nc.sync.dma_start(out=xh[:, 0:IN], in_=input_)
 
-        words = [keep.tile([P, NG], U32, align_bytes=64, name="words%d" % g) for g in range(PASSES)]
+        words = keep.tile([P, PASSES, NG], U32, align_bytes=64)
 
-        def load(g, lo, hi):
-            src, k = (W_ih_words, g) if g < PASSES_IH else (W_hh_words, g - PASSES_IH)
+        def load(g_lo, g_hi, lo, hi):
+            src, shift = (W_ih_words, 0) if g_lo < PASSES_IH else (W_hh_words, PASSES_IH)
             nc.sync.dma_start(
-                out=words[g][:, lo:hi].bitcast(I32),
-                in_=src.rearrange("g p n t -> g p (n t)")[k, :, 4 * lo : 4 * hi].bitcast(I32),
+                out=words[:, g_lo:g_hi, lo:hi].bitcast(I32),
+                in_=src.rearrange("g p n t -> p g (n t)")[:, g_lo - shift : g_hi - shift, 4 * lo : 4 * hi].bitcast(I32),
             )
 
         for half in ((2, 3), (0, 1)):
@@ -69,24 +76,21 @@ def tile_qlstmcell_w_kernel(
                         out=planes[32 * q : 32 * q + rows, :].bitcast(I32),
                         in_=scales[:, 4 * q : 4 * q + 4, :].bitcast(I32),
                     )
-        nc.vector.tensor_copy(out=words[0][64:96, 0:1].bitcast(I32), in_=planes_ih[64:96, 0:4].bitcast(I32))
-        load(0, 0, NG)
+        nc.vector.tensor_copy(out=words[64:96, 0, 0:1].bitcast(I32), in_=planes_ih[64:96, 0:4].bitcast(I32))
+        load(0, 1, 0, NG)
         nc.sync.dma_start(out=xh[:, IN : IN + H], in_=h_0)
         nc.sync.dma_start(out=bias[0:1, :], in_=b_hh.rearrange("(o n) -> o n", o=1))
         c0_sb = keep.tile([P, H], BF16)
         nc.sync.dma_start(out=c0_sb[:], in_=c_0)
-        for g in range(1, PASSES_IH):
-            load(g, 0, NG)
-        for g in range(PASSES_IH, PASSES):
-            load(g, COL_F, COL_F + 2 * H)
-        for g in range(PASSES_IH, PASSES - 1):
-            load(g, COL_O, COL_O + 2 * H)
+        for base, width in ((COL_F, 2 * H), (COL_G, H)):
+            for g in range(1, PASSES):
+                load(g, g + 1, base, base + width)
         pieces = [(0, BANK), (BANK, BANK), (2 * BANK, 256), (2 * BANK + 256, 256)]
-        last = PASSES - 1
-        load(last, COL_G, COL_G + H)
-        load(last, COL_O, COL_O + 2 * BANK)
+        load(1, PASSES_IH, COL_O, COL_O + 2 * BANK)
+        load(PASSES_IH, PASSES, COL_O, COL_O + 2 * BANK)
+        load(1, PASSES_IH, COL_O + 2 * BANK, COL_O + H)
         for off, n in pieces[2:]:
-            load(last, COL_O + off, COL_O + off + n)
+            load(PASSES_IH, PASSES, COL_O + off, COL_O + off + n)
 
         xh_words = xh[:].bitcast(F32)
         grouped = keep.tile([P, PASSES, B, 4], BF16, align_bytes=64, tag="grouped_then_th")
@@ -111,10 +115,18 @@ def tile_qlstmcell_w_kernel(
                 in_=grouped[:, first : first + n].rearrange("p g r t -> p (g r t)"),
             )
 
-        for c in range(0, NG, BANK):
-            pb = psum.tile([P, BANK], F32, tag="bank")
-            nc.tensor.matmul(out=pb[:], lhsT=ones[:], rhs=bias[:, c : c + BANK], start=True, stop=True)
-            nc.scalar.copy(out=bias[:, c : c + BANK], in_=pb[:])
+        line_o = keep.tile([P, H], F32)
+        for base in (COL_F, COL_I, COL_G, COL_O):
+            for c in range(base, base + H, BANK):
+                pb = psum.tile([P, BANK], F32, tag="bank")
+                nc.tensor.matmul(out=pb[:], lhsT=ones[:], rhs=bias[:, c : c + BANK], start=True, stop=True)
+                if base == COL_O:
+                    nc.vector.tensor_scalar(
+                        out=line_o[:, c - base : c - base + BANK], in0=pb[:], scalar1=1.0 / 6.0, scalar2=0.5,
+                        op0=ALU.mult, op1=ALU.add,
+                    )
+                else:
+                    nc.scalar.copy(out=bias[:, c : c + BANK], in_=pb[:])
 
         def mx_pass(acc, g, col, n):
             planes = planes_ih if g < PASSES_IH else planes_hh
@@ -123,7 +135,7 @@ def tile_qlstmcell_w_kernel(
                 out=acc[:, 0:n],
                 lhsT=xq[:, g, :].bitcast(FP8X4),
                 lhsT_scale=xs[:, g, :],
-                rhs=words[g][:, col : col + n].bitcast(FP8X4),
+                rhs=words[:, g, col : col + n].bitcast(FP8X4),
                 rhs_scale=planes[k:P, col : col + n],
                 start=(g == 0),
                 stop=(g == PASSES - 1),
@@ -135,82 +147,97 @@ def tile_qlstmcell_w_kernel(
         def add_bias(dest, acc, col, n):
             nc.vector.tensor_tensor(out=dest, in0=acc[:, 0:n], in1=bias[:, col : col + n], op=ALU.add)
 
-        def clip(dest, src, low, high):
-            nc.vector.tensor_scalar(out=dest, in0=src, scalar1=low, scalar2=high, op0=ALU.max, op1=ALU.min)
+        def relu(dest, src, scale, offset):
+            nc.scalar.activation(out=dest, in_=src, func=ACT.Relu, scale=scale, bias=offset)
 
-        def plus_3_times(dest, gate, other):
-            nc.vector.scalar_tensor_tensor(out=dest, in0=gate, scalar=3.0, in1=other, op0=ALU.add, op1=ALU.mult)
+        def min_times(dest, src, high, other):
+            nc.vector.scalar_tensor_tensor(out=dest, in0=src, scalar=high, in1=other, op0=ALU.min, op1=ALU.mult)
 
-        six_c1 = keep.tile([P, H], F32)
+        c1 = keep.tile([P, H], F32)
         gate = keep.tile([P, H], F32)
         cols = [slice(j * BANK, (j + 1) * BANK) for j in range(3)]
 
         acc_fi = [bank() for j in range(6)]
-        acc_g = [bank() for j in range(2)]
-        for g in range(PASSES_IH):
-            for j in range(6):
-                mx_pass(acc_fi[j], g, COL_F + j * BANK, BANK)
-            for j in range(2):
-                mx_pass(acc_g[j], g, COL_G + j * BANK, BANK)
-        for g in range(PASSES_IH, PASSES):
+        for g in range(PASSES):
             for j in range(6):
                 mx_pass(acc_fi[j], g, COL_F + j * BANK, BANK)
         for j in range(3):
-            add_bias(six_c1[:, cols[j]], acc_fi[j], COL_F + j * BANK, BANK)
+            add_bias(c1[:, cols[j]], acc_fi[j], COL_F + j * BANK, BANK)
+            relu(c1[:, cols[j]], c1[:, cols[j]], 1.0 / 6.0, 0.5)
         for j in range(3):
             add_bias(gate[:, cols[j]], acc_fi[3 + j], COL_I + j * BANK, BANK)
+            relu(gate[:, cols[j]], gate[:, cols[j]], 1.0 / 6.0, 0.5)
         for j in range(3):
-            clip(six_c1[:, cols[j]], six_c1[:, cols[j]], -3.0, 3.0)
+            min_times(c1[:, cols[j]], c1[:, cols[j]], 1.0, c0_sb[:, cols[j]])
         for j in range(3):
-            clip(gate[:, cols[j]], gate[:, cols[j]], -3.0, 3.0)
+            nc.vector.tensor_scalar(
+                out=gate[:, cols[j]], in0=gate[:, cols[j]], scalar1=1.0, scalar2=None, op0=ALU.min
+            )
         for j in range(3):
-            plus_3_times(six_c1[:, cols[j]], six_c1[:, cols[j]], c0_sb[:, cols[j]])
-
-        acc_g.append(bank())
-        for g in range(PASSES_IH):
-            mx_pass(acc_g[2], g, COL_G + 2 * BANK, BANK)
-        acc_o = []
-        for off, n in pieces:
-            acc_o.append(bank())
-            for g in range(PASSES_IH):
-                mx_pass(acc_o[-1], g, COL_O + off, n)
-        for g in range(PASSES_IH, PASSES):
-            for j in range(3):
-                mx_pass(acc_g[j], g, COL_G + j * BANK, BANK)
-            for j in range(4):
-                mx_pass(acc_o[j], g, COL_O + pieces[j][0], pieces[j][1])
+            nc.vector.tensor_tensor(
+                out=c1[:, cols[j]], in0=c1[:, cols[j]], in1=gate[:, cols[j]], op=ALU.subtract
+            )
 
         gg = keep.tile([P, H], F32, align_bytes=64, tag="x_then_g")
         th = keep.tile([P, H], F32, align_bytes=64, tag="grouped_then_th")
-        c1 = keep.tile([P, H], F32)
+        acc_g = [bank() for j in range(3)]
+        for g in range(PASSES):
+            for j in range(3):
+                mx_pass(acc_g[j], g, COL_G + j * BANK, BANK)
         for j in range(3):
             add_bias(gg[:, cols[j]], acc_g[j], COL_G + j * BANK, BANK)
+            relu(gg[:, cols[j]], gg[:, cols[j]], 1.0, 1.0)
         for j in range(3):
-            clip(gg[:, cols[j]], gg[:, cols[j]], -1.0, 1.0)
+            min_times(gg[:, cols[j]], gg[:, cols[j]], 2.0, gate[:, cols[j]])
         for j in range(3):
-            plus_3_times(gg[:, cols[j]], gate[:, cols[j]], gg[:, cols[j]])
-        for j in range(3):
-            nc.vector.tensor_tensor(
-                out=six_c1[:, cols[j]], in0=six_c1[:, cols[j]], in1=gg[:, cols[j]], op=ALU.add
-            )
-        for j in range(3):
-            nc.scalar.activation(out=c1[:, cols[j]], in_=six_c1[:, cols[j]], func=ACT.Copy, scale=1.0 / 6.0)
-        for j in range(3):
-            clip(th[:, cols[j]], six_c1[:, cols[j]], -6.0, 6.0)
-        for j in range(3):
-            nc.scalar.activation(out=th[:, cols[j]], in_=th[:, cols[j]], func=ACT.Copy, scale=1.0 / 36.0)
+            nc.vector.tensor_tensor(out=c1[:, cols[j]], in0=c1[:, cols[j]], in1=gg[:, cols[j]], op=ALU.add)
+            relu(th[:, cols[j]], c1[:, cols[j]], 1.0, 1.0)
         nc.sync.dma_start(out=out_1, in_=c1[:])
 
-        def o_step(step, j):
-            off, n = pieces[j]
-            s = slice(off, off + n)
-            if step == 0:
-                add_bias(gate[:, s], acc_o[j], COL_O + off, n)
-            elif step == 1:
-                clip(gate[:, s], gate[:, s], -3.0, 3.0)
-            else:
-                plus_3_times(gate[:, s], gate[:, s], th[:, s])
-                nc.sync.dma_start(out=out_0[:, s], in_=gate[:, s])
+        acc_o = [bank() for j in range(4)]
+        for some in ((0, 1), (2, 3)):
+            for g in range(PASSES_IH):
+                for j in some:
+                    mx_pass(acc_o[j], g, COL_O + pieces[j][0], pieces[j][1])
+            for j in some:
+                for g in range(PASSES_IH, PASSES):
+                    mx_pass(acc_o[j], g, COL_O + pieces[j][0], pieces[j][1])
 
-        for step, j in ((0, 0), (0, 1), (1, 0), (1, 1), (2, 0), (2, 1), (0, 2), (1, 2), (0, 3), (2, 2), (1, 3), (2, 3)):
-            o_step(step, j)
+        part = [slice(off, off + n) for off, n in pieces]
+
+        def o_line(j):
+            off, n = pieces[j]
+            nc.vector.scalar_tensor_tensor(
+                out=gate[:, part[j]], in0=acc_o[j][:, 0:n], scalar=1.0 / 6.0, in1=line_o[:, part[j]],
+                op0=ALU.mult, op1=ALU.add,
+            )
+
+        def th_end(j):
+            nc.vector.tensor_scalar(
+                out=th[:, cols[j]], in0=th[:, cols[j]], scalar1=2.0, scalar2=-1.0, op0=ALU.min, op1=ALU.add
+            )
+
+        def o_clip(j):
+            nc.vector.tensor_scalar(
+                out=gate[:, part[j]], in0=gate[:, part[j]], scalar1=0.0, scalar2=1.0, op0=ALU.max, op1=ALU.min
+            )
+
+        def o_store(j):
+            nc.sync.dma_start(out=out_0[:, part[j]], in_=gate[:, part[j]])
+
+        for j in range(3):
+            th_end(j)
+        for j in range(2):
+            o_line(j)
+            relu(gate[:, part[j]], gate[:, part[j]], 1.0, 0.0)
+        for j in range(2):
+            min_times(gate[:, part[j]], gate[:, part[j]], 1.0, th[:, part[j]])
+            o_store(j)
+        o_line(2)
+        o_clip(2)
+        o_line(3)
+        for j in (2, 3):
+            if j == 3:
+                o_clip(3)
+            nc.vector.tensor_tensor(out=gate[:, part[j]], in0=gate[:, part[j]], in1=th[:, part[j]], op=ALU.mult)
+            o_store(j)

@@ -76,12 +76,11 @@ def tile_qlstmcell_w_kernel(
                         out=planes[32 * q : 32 * q + rows, :].bitcast(I32),
                         in_=scales[:, 4 * q : 4 * q + 4, :].bitcast(I32),
                     )
-        nc.vector.tensor_copy(out=words[64:96, 0, 0:1].bitcast(I32), in_=planes_ih[64:96, 0:4].bitcast(I32))
-        load(0, 1, 0, NG)
         nc.sync.dma_start(out=xh[:, IN : IN + H], in_=h_0)
         nc.sync.dma_start(out=bias[0:1, :], in_=b_hh.rearrange("(o n) -> o n", o=1))
         c0_sb = keep.tile([P, H], BF16)
         nc.sync.dma_start(out=c0_sb[:], in_=c_0)
+        load(0, 1, 0, NG)
         for base, width in ((COL_F, 2 * H), (COL_G, H)):
             for g in range(1, PASSES):
                 load(g, g + 1, base, base + width)

@@ -80,16 +80,19 @@ def tile_qlstmcell_w_kernel(
         nc.sync.dma_start(out=bias[0:1, :], in_=b_hh.rearrange("(o n) -> o n", o=1))
         c0_sb = keep.tile([P, H], BF16)
         nc.sync.dma_start(out=c0_sb[:], in_=c_0)
-        load(0, 1, 0, NG)
-        for base, width in ((COL_F, 2 * H), (COL_G, H)):
-            for g in range(1, PASSES):
-                load(g, g + 1, base, base + width)
+        load(0, 1, 0, COL_O + 2 * BANK)
+        for g in range(1, PASSES):
+            load(g, g + 1, COL_F, COL_F + 2 * H)
+        for g in range(PASSES):
+            load(g, g + 1, COL_G, COL_G + H)
         pieces = [(0, BANK), (BANK, BANK), (2 * BANK, 256), (2 * BANK + 256, 256)]
         load(1, PASSES_IH, COL_O, COL_O + 2 * BANK)
-        load(PASSES_IH, PASSES, COL_O, COL_O + 2 * BANK)
-        load(1, PASSES_IH, COL_O + 2 * BANK, COL_O + H)
-        for off, n in pieces[2:]:
-            load(PASSES_IH, PASSES, COL_O + off, COL_O + off + n)
+        for g in range(PASSES_IH, PASSES):
+            load(g, g + 1, COL_O, COL_O + 2 * BANK)
+        load(0, PASSES_IH, COL_O + 2 * BANK, COL_O + H)
+        load(PASSES_IH, PASSES, COL_O + 2 * BANK, COL_O + 2 * BANK + 256)
+        load(PASSES_IH, PASSES - 1, COL_O + 2 * BANK + 256, COL_O + H)
+        load(PASSES - 1, PASSES, COL_O + 2 * BANK + 256, COL_O + H)
 
         xh_words = xh[:].bitcast(F32)
         grouped = keep.tile([P, PASSES, B, 4], BF16, align_bytes=64, tag="grouped_then_th")
@@ -194,13 +197,15 @@ def tile_qlstmcell_w_kernel(
         nc.sync.dma_start(out=out_1, in_=c1[:])
 
         acc_o = [bank() for j in range(4)]
-        for some in ((0, 1), (2, 3)):
-            for g in range(PASSES_IH):
+        def o_passes(some, g_lo, g_hi):
+            for g in range(g_lo, g_hi):
                 for j in some:
                     mx_pass(acc_o[j], g, COL_O + pieces[j][0], pieces[j][1])
-            for j in some:
-                for g in range(PASSES_IH, PASSES):
-                    mx_pass(acc_o[j], g, COL_O + pieces[j][0], pieces[j][1])
+
+        o_passes((0, 1), 0, PASSES)
+        o_passes((2, 3), 0, PASSES_IH)
+        o_passes((2,), PASSES_IH, PASSES)
+        o_passes((3,), PASSES_IH, PASSES)
 
         part = [slice(off, off + n) for off, n in pieces]
 

@@ -80,19 +80,17 @@ def tile_qlstmcell_w_kernel(
         nc.sync.dma_start(out=bias[0:1, :], in_=b_hh.rearrange("(o n) -> o n", o=1))
         c0_sb = keep.tile([P, H], BF16)
         nc.sync.dma_start(out=c0_sb[:], in_=c_0)
-        load(0, 1, 0, COL_O + 2 * BANK)
+        load(0, 1, 0, NG)
         for g in range(1, PASSES):
             load(g, g + 1, COL_F, COL_F + 2 * H)
-        for g in range(PASSES):
+        for g in range(1, PASSES):
             load(g, g + 1, COL_G, COL_G + H)
-        pieces = [(0, BANK), (BANK, BANK), (2 * BANK, 256), (2 * BANK + 256, 256)]
-        load(1, PASSES_IH, COL_O, COL_O + 2 * BANK)
-        for g in range(PASSES_IH, PASSES):
+        pieces = [(0, BANK), (BANK, BANK), (2 * BANK, BANK)]
+        for g in range(1, PASSES):
             load(g, g + 1, COL_O, COL_O + 2 * BANK)
-        load(0, PASSES_IH, COL_O + 2 * BANK, COL_O + H)
-        load(PASSES_IH, PASSES, COL_O + 2 * BANK, COL_O + 2 * BANK + 256)
-        load(PASSES_IH, PASSES - 1, COL_O + 2 * BANK + 256, COL_O + H)
-        load(PASSES - 1, PASSES, COL_O + 2 * BANK + 256, COL_O + H)
+        load(1, PASSES_IH, COL_O + 2 * BANK, COL_O + H)
+        load(PASSES_IH, PASSES - 1, COL_O + 2 * BANK, COL_O + H)
+        load(PASSES - 1, PASSES, COL_O + 2 * BANK, COL_O + H)
 
         xh_words = xh[:].bitcast(F32)
         grouped = keep.tile([P, PASSES, B, 4], BF16, align_bytes=64, tag="grouped_then_th")
@@ -196,16 +194,14 @@ def tile_qlstmcell_w_kernel(
             relu(th[:, cols[j]], c1[:, cols[j]], 1.0, 1.0)
         nc.sync.dma_start(out=out_1, in_=c1[:])
 
-        acc_o = [bank() for j in range(4)]
+        acc_o = [bank() for j in range(3)]
         def o_passes(some, g_lo, g_hi):
             for g in range(g_lo, g_hi):
                 for j in some:
                     mx_pass(acc_o[j], g, COL_O + pieces[j][0], pieces[j][1])
 
         o_passes((0, 1), 0, PASSES)
-        o_passes((2, 3), 0, PASSES_IH)
-        o_passes((2,), PASSES_IH, PASSES)
-        o_passes((3,), PASSES_IH, PASSES)
+        o_passes((2,), 0, PASSES)
 
         part = [slice(off, off + n) for off, n in pieces]
 
@@ -221,11 +217,6 @@ def tile_qlstmcell_w_kernel(
                 out=th[:, cols[j]], in0=th[:, cols[j]], scalar1=2.0, scalar2=-1.0, op0=ALU.min, op1=ALU.add
             )
 
-        def o_clip(j):
-            nc.vector.tensor_scalar(
-                out=gate[:, part[j]], in0=gate[:, part[j]], scalar1=0.0, scalar2=1.0, op0=ALU.max, op1=ALU.min
-            )
-
         def o_store(j):
             nc.sync.dma_start(out=out_0[:, part[j]], in_=gate[:, part[j]])
 
@@ -237,11 +228,16 @@ def tile_qlstmcell_w_kernel(
         for j in range(2):
             min_times(gate[:, part[j]], gate[:, part[j]], 1.0, th[:, part[j]])
             o_store(j)
-        o_line(2)
-        o_clip(2)
-        o_line(3)
-        for j in (2, 3):
-            if j == 3:
-                o_clip(3)
-            nc.vector.tensor_tensor(out=gate[:, part[j]], in0=gate[:, part[j]], in1=th[:, part[j]], op=ALU.mult)
-            o_store(j)
+        halves = [slice(2 * BANK, 2 * BANK + 256), slice(2 * BANK + 256, H)]
+        for j, s in enumerate(halves):
+            nc.vector.scalar_tensor_tensor(
+                out=gate[:, s], in0=acc_o[2][:, 256 * j : 256 * (j + 1)], scalar=1.0 / 6.0, in1=line_o[:, s],
+                op0=ALU.mult, op1=ALU.add,
+            )
+        for s in halves:
+            nc.vector.tensor_scalar(
+                out=gate[:, s], in0=gate[:, s], scalar1=0.0, scalar2=1.0, op0=ALU.max, op1=ALU.min
+            )
+        for s in halves:
+            nc.vector.tensor_tensor(out=gate[:, s], in0=gate[:, s], in1=th[:, s], op=ALU.mult)
+            nc.sync.dma_start(out=out_0[:, s], in_=gate[:, s])

@@ -81,16 +81,18 @@ def tile_qlstmcell_w_kernel(
         c0_sb = keep.tile([P, H], BF16)
         nc.sync.dma_start(out=c0_sb[:], in_=c_0)
         load(0, 1, 0, NG)
-        for g in range(1, PASSES):
+        load(1, 2, 0, COL_O + 2 * BANK)
+        for g in range(2, PASSES):
             load(g, g + 1, COL_F, COL_F + 2 * H)
         for g in range(1, PASSES):
             load(g, g + 1, COL_G, COL_G + H)
-        pieces = [(0, BANK), (BANK, BANK), (2 * BANK, BANK)]
-        for g in range(1, PASSES):
+        pieces = [(0, BANK), (BANK, BANK), (2 * BANK, 256), (2 * BANK + 256, 256)]
+        for g in range(2, PASSES):
             load(g, g + 1, COL_O, COL_O + 2 * BANK)
         load(1, PASSES_IH, COL_O + 2 * BANK, COL_O + H)
         load(PASSES_IH, PASSES - 1, COL_O + 2 * BANK, COL_O + H)
-        load(PASSES - 1, PASSES, COL_O + 2 * BANK, COL_O + H)
+        for off, n in pieces[2:]:
+            load(PASSES - 1, PASSES, COL_O + off, COL_O + off + n)
 
         xh_words = xh[:].bitcast(F32)
         grouped = keep.tile([P, PASSES, B, 4], BF16, align_bytes=64, tag="grouped_then_th")
@@ -191,17 +193,16 @@ def tile_qlstmcell_w_kernel(
             min_times(gg[:, cols[j]], gg[:, cols[j]], 2.0, gate[:, cols[j]])
         for j in range(3):
             nc.vector.tensor_tensor(out=c1[:, cols[j]], in0=c1[:, cols[j]], in1=gg[:, cols[j]], op=ALU.add)
-            relu(th[:, cols[j]], c1[:, cols[j]], 1.0, 1.0)
         nc.sync.dma_start(out=out_1, in_=c1[:])
 
-        acc_o = [bank() for j in range(3)]
+        acc_o = [bank() for j in range(4)]
         def o_passes(some, g_lo, g_hi):
             for g in range(g_lo, g_hi):
                 for j in some:
                     mx_pass(acc_o[j], g, COL_O + pieces[j][0], pieces[j][1])
 
         o_passes((0, 1), 0, PASSES)
-        o_passes((2,), 0, PASSES)
+        o_passes((2, 3), 0, PASSES)
 
         part = [slice(off, off + n) for off, n in pieces]
 
@@ -212,32 +213,28 @@ def tile_qlstmcell_w_kernel(
                 op0=ALU.mult, op1=ALU.add,
             )
 
-        def th_end(j):
+        def th_clip(j):
             nc.vector.tensor_scalar(
-                out=th[:, cols[j]], in0=th[:, cols[j]], scalar1=2.0, scalar2=-1.0, op0=ALU.min, op1=ALU.add
+                out=th[:, cols[j]], in0=c1[:, cols[j]], scalar1=-1.0, scalar2=1.0, op0=ALU.max, op1=ALU.min
             )
 
         def o_store(j):
             nc.sync.dma_start(out=out_0[:, part[j]], in_=gate[:, part[j]])
 
         for j in range(3):
-            th_end(j)
+            th_clip(j)
         for j in range(2):
             o_line(j)
             relu(gate[:, part[j]], gate[:, part[j]], 1.0, 0.0)
         for j in range(2):
             min_times(gate[:, part[j]], gate[:, part[j]], 1.0, th[:, part[j]])
             o_store(j)
-        halves = [slice(2 * BANK, 2 * BANK + 256), slice(2 * BANK + 256, H)]
-        for j, s in enumerate(halves):
-            nc.vector.scalar_tensor_tensor(
-                out=gate[:, s], in0=acc_o[2][:, 256 * j : 256 * (j + 1)], scalar=1.0 / 6.0, in1=line_o[:, s],
-                op0=ALU.mult, op1=ALU.add,
-            )
-        for s in halves:
+        for j in (2, 3):
+            o_line(j)
+        for s in part[2:]:
             nc.vector.tensor_scalar(
                 out=gate[:, s], in0=gate[:, s], scalar1=0.0, scalar2=1.0, op0=ALU.max, op1=ALU.min
             )
-        for s in halves:
+        for s in part[2:]:
             nc.vector.tensor_tensor(out=gate[:, s], in0=gate[:, s], in1=th[:, s], op=ALU.mult)
             nc.sync.dma_start(out=out_0[:, s], in_=gate[:, s])

from contextlib import ExitStack

import concourse.mybir as mybir
from concourse.masks import make_identity

F32 = mybir.dt.float32
BF16 = mybir.dt.bfloat16
I32 = mybir.dt.int32
U32 = mybir.dt.uint32
U8 = mybir.dt.uint8
FP8X4 = mybir.dt.float8_e4m3fn_x4
ALU = mybir.AluOpType
ACT = mybir.ActivationFunctionType

P = 128
B = 128
IN = 2048
H = 1536
NG = 4 * H
PASSES_IH = IN // 512
PASSES_HH = H // 512
PASSES = PASSES_IH + PASSES_HH
BANK = 512
FLOPS = 2 * B * (IN + H) * NG

COL_F, COL_I, COL_O, COL_G = 0, H, 2 * H, 3 * H


def tile_qlstmcell_w_kernel(
    tc, input_, h_0, c_0, W_ih_words, W_ih_scales, W_hh_words, W_hh_scales, b_hh, out_0, out_1
):
    nc = tc.nc
    with ExitStack() as ctx:
        keep = ctx.enter_context(tc.tile_pool(name="keep", bufs=1))
        psum = ctx.enter_context(tc.psum_pool(name="psum", bufs=8))

        ctx.enter_context(
            tc.manual_schedule(
                engines={
                    mybir.EngineType.SP,
                    mybir.EngineType.DVE,
                    mybir.EngineType.PE,
                    mybir.EngineType.Activation,
                }
            )
        )

        ident = keep.tile([P, P], F32)
        make_identity(nc, ident[:])

        planes_ih = keep.tile([P, NG], U8, align_bytes=64)
        planes_hh = keep.tile([P, NG], U8, align_bytes=64)
        nc.vector.memset(planes_ih[:].bitcast(I32), 0)
        nc.vector.memset(planes_hh[:].bitcast(I32), 0)
        bias = keep.tile([P, NG], BF16)
        nc.vector.memset(bias[:].bitcast(I32), 0)
        ones = keep.tile([P, P], BF16)
        nc.vector.memset(ones[:], 1.0)

        xh = keep.tile([P, IN + H], BF16, align_bytes=64, tag="x_then_g")
        nc.sync.dma_start(out=xh[:, 0:IN], in_=input_)

        words = keep.tile([P, PASSES, NG], U32, align_bytes=64)

        def load(g_lo, g_hi, lo, hi):
            src, shift = (W_ih_words, 0) if g_lo < PASSES_IH else (W_hh_words, PASSES_IH)
            nc.sync.dma_start(
                out=words[:, g_lo:g_hi, lo:hi].bitcast(I32),
                in_=src.rearrange("g p n t -> p g (n t)")[:, g_lo - shift : g_hi - shift, 4 * lo : 4 * hi].bitcast(I32),
            )

        for half in ((2, 3), (0, 1)):
            for planes, scales, rows in ((planes_ih, W_ih_scales, 16), (planes_hh, W_hh_scales, 12)):
                for q in half:
                    nc.sync.dma_start(
                        out=planes[32 * q : 32 * q + rows, :].bitcast(I32),
                        in_=scales[:, 4 * q : 4 * q + 4, :].bitcast(I32),
                    )
        nc.sync.dma_start(out=xh[:, IN : IN + H], in_=h_0)
        nc.sync.dma_start(out=bias[0:1, :], in_=b_hh.rearrange("(o n) -> o n", o=1))
        c0_sb = keep.tile([P, H], BF16)
        nc.sync.dma_start(out=c0_sb[:], in_=c_0)
        load(0, 1, 0, NG)
        load(1, 2, 0, COL_O + 2 * BANK)
        for g in range(2, PASSES):
            load(g, g + 1, COL_F, COL_F + 2 * H)
        for g in range(1, PASSES):
            load(g, g + 1, COL_G, COL_G + H)
        pieces = [(0, BANK), (BANK, BANK), (2 * BANK, 256), (2 * BANK + 256, 256)]
        for g in range(2, PASSES):
            load(g, g + 1, COL_O, COL_O + 2 * BANK)
        load(1, PASSES_IH, COL_O + 2 * BANK, COL_O + H)
        load(PASSES_IH, PASSES - 1, COL_O + 2 * BANK, COL_O + H)
        for off, n in pieces[2:]:
            load(PASSES - 1, PASSES, COL_O + off, COL_O + off + n)

        xh_words = xh[:].bitcast(F32)
        grouped = keep.tile([P, PASSES, B, 4], BF16, align_bytes=64, tag="grouped_then_th")
        xq = keep.tile([P, PASSES, B], U32, align_bytes=64)
        xs = keep.tile([P, PASSES, B], U8, align_bytes=64)
        for first in range(0, PASSES, 2):
            n = min(2, PASSES - first)
            xt = psum.tile([P, 2, 2, B], F32, tag="bank")
            for j in range(n):
                g = first + j
                for u in range(2):
                    nc.tensor.transpose(
                        xt[:, j, u, :], xh_words[:, 256 * g + u : 256 * (g + 1) : 2], ident[:]
                    )
            nc.vector.tensor_copy(
                out=grouped[:, first : first + n].bitcast(F32),
                in_=xt[:, 0:n].rearrange("p g u r -> p g r u"),
            )
            nc.vector.quantize_mx(
                out=xq[:, first : first + n, :].rearrange("p g r -> p (g r)").bitcast(FP8X4),
                scales=xs[:, first : first + n, :].rearrange("p g r -> p (g r)"),
                in_=grouped[:, first : first + n].rearrange("p g r t -> p (g r t)"),
            )

        line_o = keep.tile([P, H], F32)
        for base in (COL_F, COL_I, COL_G, COL_O):
            for c in range(base, base + H, BANK):
                pb = psum.tile([P, BANK], F32, tag="bank")
                nc.tensor.matmul(out=pb[:], lhsT=ones[:], rhs=bias[:, c : c + BANK], start=True, stop=True)
                if base == COL_O:
                    nc.vector.tensor_scalar(
                        out=line_o[:, c - base : c - base + BANK], in0=pb[:], scalar1=1.0 / 6.0, scalar2=0.5,
                        op0=ALU.mult, op1=ALU.add,
                    )
                else:
                    nc.scalar.copy(out=bias[:, c : c + BANK], in_=pb[:])

        def mx_pass(acc, g, col, n):
            planes = planes_ih if g < PASSES_IH else planes_hh
            k = 4 * (g % PASSES_IH)
            nc.tensor.matmul_mx(
                out=acc[:, 0:n],
                lhsT=xq[:, g, :].bitcast(FP8X4),
                lhsT_scale=xs[:, g, :],
                rhs=words[:, g, col : col + n].bitcast(FP8X4),
                rhs_scale=planes[k:P, col : col + n],
                start=(g == 0),
                stop=(g == PASSES - 1),
            )

        def bank():
            return psum.tile([P, BANK], F32, tag="bank", name="acc")

        def add_bias(dest, acc, col, n):
            nc.vector.tensor_tensor(out=dest, in0=acc[:, 0:n], in1=bias[:, col : col + n], op=ALU.add)

        def relu(dest, src, scale, offset):
            nc.scalar.activation(out=dest, in_=src, func=ACT.Relu, scale=scale, bias=offset)

        def min_times(dest, src, high, other):
            nc.vector.scalar_tensor_tensor(out=dest, in0=src, scalar=high, in1=other, op0=ALU.min, op1=ALU.mult)

        c1 = keep.tile([P, H], F32)
        gate = keep.tile([P, H], F32)
        cols = [slice(j * BANK, (j + 1) * BANK) for j in range(3)]

        acc_fi = [bank() for j in range(6)]
        for g in range(PASSES):
            for j in range(6):
                mx_pass(acc_fi[j], g, COL_F + j * BANK, BANK)
        for j in range(3):
            add_bias(c1[:, cols[j]], acc_fi[j], COL_F + j * BANK, BANK)
            relu(c1[:, cols[j]], c1[:, cols[j]], 1.0 / 6.0, 0.5)
        for j in range(3):
            add_bias(gate[:, cols[j]], acc_fi[3 + j], COL_I + j * BANK, BANK)
            relu(gate[:, cols[j]], gate[:, cols[j]], 1.0 / 6.0, 0.5)
        for j in range(3):
            min_times(c1[:, cols[j]], c1[:, cols[j]], 1.0, c0_sb[:, cols[j]])
        for j in range(3):
            nc.vector.tensor_scalar(
                out=gate[:, cols[j]], in0=gate[:, cols[j]], scalar1=1.0, scalar2=None, op0=ALU.min
            )
        for j in range(3):
            nc.vector.tensor_tensor(
                out=c1[:, cols[j]], in0=c1[:, cols[j]], in1=gate[:, cols[j]], op=ALU.subtract
            )

        gg = keep.tile([P, H], F32, align_bytes=64, tag="x_then_g")
        th = keep.tile([P, H], F32, align_bytes=64, tag="grouped_then_th")
        acc_g = [bank() for j in range(3)]
        for g in range(PASSES):
            for j in range(3):
                mx_pass(acc_g[j], g, COL_G + j * BANK, BANK)
        for j in range(3):
            add_bias(gg[:, cols[j]], acc_g[j], COL_G + j * BANK, BANK)
            relu(gg[:, cols[j]], gg[:, cols[j]], 1.0, 1.0)
        for j in range(3):
            min_times(gg[:, cols[j]], gg[:, cols[j]], 2.0, gate[:, cols[j]])
        for j in range(3):
            nc.vector.tensor_tensor(out=c1[:, cols[j]], in0=c1[:, cols[j]], in1=gg[:, cols[j]], op=ALU.add)
        nc.sync.dma_start(out=out_1, in_=c1[:])

        acc_o = [bank() for j in range(4)]
        def o_passes(some, g_lo, g_hi):
            for g in range(g_lo, g_hi):
                for j in some:
                    mx_pass(acc_o[j], g, COL_O + pieces[j][0], pieces[j][1])

        o_passes((0, 1), 0, PASSES)
        o_passes((2, 3), 0, PASSES)

        part = [slice(off, off + n) for off, n in pieces]

        def o_line(j):
            off, n = pieces[j]
            nc.vector.scalar_tensor_tensor(
                out=gate[:, part[j]], in0=acc_o[j][:, 0:n], scalar=1.0 / 6.0, in1=line_o[:, part[j]],
                op0=ALU.mult, op1=ALU.add,
            )

        def th_clip(j):
            nc.vector.tensor_scalar(
                out=th[:, cols[j]], in0=c1[:, cols[j]], scalar1=-1.0, scalar2=1.0, op0=ALU.max, op1=ALU.min
            )

        def o_store(j):
            nc.sync.dma_start(out=out_0[:, part[j]], in_=gate[:, part[j]])

        for j in range(3):
            th_clip(j)
        for j in range(2):
            o_line(j)
            relu(gate[:, part[j]], gate[:, part[j]], 1.0, 0.0)
        for j in range(2):
            min_times(gate[:, part[j]], gate[:, part[j]], 1.0, th[:, part[j]])
            o_store(j)
        for j in (2, 3):
            o_line(j)
        for s in part[2:]:
            nc.vector.tensor_scalar(
                out=gate[:, s], in0=gate[:, s], scalar1=0.0, scalar2=1.0, op0=ALU.max, op1=ALU.min
            )
        for s in part[2:]:
            nc.vector.tensor_tensor(out=gate[:, s], in0=gate[:, s], in1=th[:, s], op=ALU.mult)
            nc.sync.dma_start(out=out_0[:, s], in_=gate[:, s])
